import numpy as np
import ml_dtypes


def mxq(x, axis, fmt="e4m3"):
    dtype, down = {"e4m3": (ml_dtypes.float8_e4m3fn, 7), "e5m2": (ml_dtypes.float8_e5m2, 14)}[fmt]
    v = np.moveaxis(np.asarray(x, np.float32).astype(ml_dtypes.bfloat16).astype(np.float64), axis, -1)
    blocks = v.reshape(v.shape[:-1] + (-1, 32))
    amax = np.abs(blocks).max(-1, keepdims=True)
    byte = np.maximum(np.where(amax > 0, np.frexp(amax)[1] - 1 + 127, 0) - down, 1)
    scale = np.exp2(byte - 127.0)
    codes = (blocks / scale).astype(np.float32).astype(dtype).astype(np.float64)
    return np.moveaxis((codes * scale).reshape(v.shape), -1, axis)


WIDE = False


def mx_kscale(k):
    if not WIDE:
        return np.ones(k)
    levels = np.array([10, -10, 5, -5, 0])
    if k % 512:
        return np.exp2(np.random.permutation(np.resize(levels, k // 32))).repeat(32)
    a = np.empty((k // 512, 16))
    for p in range(k // 512):
        a[p, :8] = np.random.permutation(np.resize(levels, 8))
        for g in range(8):
            far = levels[np.abs(levels - a[p, g]) >= 10]
            a[p, g + 8] = far[np.random.randint(len(far))]
    return np.exp2(a.ravel()).repeat(32)


BF16 = ml_dtypes.bfloat16


def bf(x):
    return np.asarray(x, np.float32).astype(BF16)


def f64(x):
    return np.asarray(x).astype(np.float64)


B, H, W, C, NF, ZD = 128, 4, 4, 512, 512, 512
EPS = 1e-8
LRELU_SLOPE = 0.2


def setup_inputs():
    s = mx_kscale(C)
    return {"x": bf(np.random.standard_normal((B, H, W, C)) * s),
            "dlatents": bf(np.random.standard_normal((B, ZD))),
            "noise_map": bf(np.random.standard_normal((B, H, W, 1))),
            "conv_w": bf(np.random.standard_normal((C, NF)) / np.sqrt(C) / s[:, None]),
            "noise_weight": bf(np.random.standard_normal((1, 1, 1, NF)) * 0.5),
            "bias": bf(np.random.standard_normal((1, 1, 1, NF)) * 0.5),
            "dense_w": bf(np.random.standard_normal((ZD, 2 * NF)) / np.sqrt(ZD)),
            "dense_b": bf(np.random.standard_normal(2 * NF) * 0.3)}


def reference(x, dlatents, noise_map, conv_w, noise_weight, bias, dense_w, dense_b):
    y = mxq(f64(x), 3, "e4m3") @ mxq(f64(conv_w), 0, "e4m3")
    y = y + f64(noise_weight) * f64(noise_map) + f64(bias)
    y = np.where(y >= 0.0, y, LRELU_SLOPE * y)
    mu = np.mean(y, axis=(1, 2), keepdims=True)
    var = np.mean(np.square(y - mu), axis=(1, 2), keepdims=True)
    yn = (y - mu) / np.sqrt(var + EPS)
    gb = f64(dlatents) @ f64(dense_w) + f64(dense_b)
    nf = y.shape[-1]
    gb = gb.reshape(-1, 2, 1, 1, nf)
    gamma, beta = gb[:, 0], gb[:, 1]
    return yn * (1.0 + gamma) + beta

@@ -1,0 +1,409 @@
+from contextlib import ExitStack
+
+import concourse.mybir as mybir
+from concourse.masks import make_identity
+
+FLOPS = 2 * 2048 * 512 * 512 + 2 * 128 * 512 * 1024
+
+F32 = mybir.dt.float32
+BF16 = mybir.dt.bfloat16
+U32 = mybir.dt.uint32
+U8 = mybir.dt.uint8
+I32 = mybir.dt.int32
+FP8X4 = mybir.dt.float8_e4m3fn_x4
+ALU = mybir.AluOpType
+ACT = mybir.ActivationFunctionType
+
+P = 128
+HW = 16
+NG = 4
+NCT = 4
+NSTEP = NG * NCT
+EPS = 1e-8
+SLOPE = 0.2
+LAG = 8
+USE_SG = True
+
+
+def tile_styleganlayerepilogue_kernel(
+    tc, x, dlatents, noise_map, conv_w, noise_weight, bias, dense_w, dense_b, out
+):
+    nc = tc.nc
+    with ExitStack() as ctx:
+        keep = ctx.enter_context(tc.tile_pool(name="keep", bufs=1))
+        work = ctx.enter_context(tc.tile_pool(name="work", bufs=3))
+        small = ctx.enter_context(tc.tile_pool(name="small", bufs=2))
+        ps = ctx.enter_context(tc.psum_pool(name="ps", bufs=1))
+
+        rows = keep.tile([P, P], BF16, name="rows")
+        nc.vector.memset(rows[:].bitcast(I32), 0)
+        warm = keep.tile([P, 1], F32, name="warm")
+        nc.vector.memset(warm[:], 1.0)
+        ident_b = keep.tile([P, P], BF16, name="ident_b")
+        make_identity(nc, ident_b[:])
+        ident_f = keep.tile([P, P], F32, name="ident_f")
+        make_identity(nc, ident_f[:])
+        warm2 = keep.tile([P, 1], F32, name="warm2")
+        eps_t = keep.tile([P, 1], F32, name="eps_t")
+        nc.vector.memset(eps_t[:], EPS)
+
+        xv = x.rearrange("b h w c -> b (h w c)")
+        x_sb = [keep.tile([P, 2048], BF16, name="x_sb%d" % g) for g in range(NG)]
+        w_raw = keep.tile([P, 4, 512], BF16, name="w_raw")
+        nm_sb = keep.tile([P, HW], BF16, name="nm_sb")
+        dl_sb = keep.tile([P, 512], BF16, name="dl_sb")
+        dw_sb = keep.tile([P, 4, 1024], BF16, name="dw_sb")
+
+        nc.sync.dma_start(out=nm_sb[:], in_=noise_map.rearrange("b h w o -> b (h w o)"))
+        nc.sync.dma_start(
+            out=rows[0:4, :], in_=noise_weight.rearrange("a b c (r n) -> (a b c r) n", r=4)
+        )
+        nc.sync.dma_start(out=rows[4:8, :], in_=bias.rearrange("a b c (r n) -> (a b c r) n", r=4))
+        nc.scalar.activation(out=warm2[:], in_=warm[:], func=ACT.Abs_reciprocal_sqrt)
+        nc.sync.dma_start(out=x_sb[0][:], in_=xv[:, 0:2048])
+        nc.sync.dma_start(
+            out=w_raw[:],
+            in_=conv_w.rearrange("(p j) c -> p j c", j=4),
+        )
+        for g in range(1, NG):
+            nc.sync.dma_start(out=x_sb[g][:], in_=xv[:, g * 2048 : (g + 1) * 2048])
+        nc.sync.dma_start(out=dl_sb[:], in_=dlatents)
+        nc.sync.dma_start(out=dw_sb[:], in_=dense_w.rearrange("(k p) n -> p k n", p=P))
+        db_bc = keep.tile([P, 1024], BF16, name="db_bc")
+        nc.sync.dma_start(out=db_bc[:], in_=dense_b.partition_broadcast(P))
+
+        cols_ps = ps.tile([P, P], BF16, name="cols_ps", tag="a", bufs=2)
+        nc.tensor.transpose(cols_ps[:], rows[:], ident_b[:])
+        cols = keep.tile([P, 8], F32, name="cols")
+        nc.vector.tensor_copy(out=cols[:], in_=cols_ps[:, 0:8])
+
+
+        nm_bc = [keep.tile([P, 1024], BF16, name="nm_bc%d" % h) for h in range(2)]
+        t_add = {}
+
+        def noise_half(half):
+            nm_ps = ps.tile([P, 1024], BF16, name="nm_ps%d" % half, tag=("sy" if half == 0 else "sq"))
+            for j in range(8):
+                hw = half * 8 + j
+                nc.tensor.matmul(
+                    out=nm_ps[:, j * P : (j + 1) * P],
+                    lhsT=nm_sb[:, hw : hw + 1].to_broadcast([P, P]),
+                    rhs=ident_b[:],
+                    start=True,
+                    stop=True,
+                )
+            nc.scalar.copy(out=nm_bc[half][:], in_=nm_ps[:])
+
+        def noise_term(s):
+            ct, g = s // NG, s % NG
+            t_add[s] = keep.tile([P, 512], F32, name="t_add%d" % s)
+            nc.gpsimd.tensor_scalar(
+                out=t_add[s][:],
+                in0=nm_bc[g // 2][:, (g % 2) * 512 : (g % 2 + 1) * 512],
+                scalar1=cols[:, ct : ct + 1],
+                scalar2=cols[:, 4 + ct : 5 + ct],
+                op0=ALU.mult,
+                op1=ALU.add,
+            )
+
+        def noise_term_s(s):
+            ct, g = s // NG, s % NG
+            t_add[s] = keep.tile([P, 512], F32, name="t_add%d" % s)
+            nc.scalar.activation(
+                out=t_add[s][:],
+                in_=nm_bc[g // 2][:, (g % 2) * 512 : (g % 2 + 1) * 512],
+                func=ACT.Identity,
+                bias=cols[:, 4 + ct : 5 + ct],
+                scale=cols[:, ct : ct + 1],
+            )
+
+        w_grp = keep.tile([P, 512, 4], BF16, name="w_grp", align_bytes=64)
+        w_codes = keep.tile([P, 512], U32, name="w_codes", align_bytes=64)
+        w_scales = keep.tile([P, 512], U8, name="w_scales", align_bytes=64)
+
+        def w_quant():
+            nc.vector.tensor_copy(out=w_grp[:], in_=w_raw[:].rearrange("p t c -> p c t"))
+            nc.vector.quantize_mx(
+                out=w_codes[:].bitcast(FP8X4),
+                scales=w_scales[:],
+                in_=w_grp[:].rearrange("p c t -> p (c t)"),
+            )
+
+        x_grp = [keep.tile([P, 2048], BF16, name="x_grp%d" % g, align_bytes=64) for g in range(NG)]
+        x_codes = [keep.tile([P, 512], U32, name="x_codes%d" % g, align_bytes=64) for g in range(NG)]
+        x_scales = [keep.tile([P, 512], U8, name="x_scales%d" % g, align_bytes=64) for g in range(NG)]
+        outv = out.rearrange("b h w c -> b (h w) c")
+        acc_t = {}
+        z_t = {}
+        y_t = {}
+        q_t = {}
+        w_t = {}
+        sum_t = {}
+        st_t = {}
+        sm = {}
+        gb_sb = [keep.tile([P, 512], F32, name="gb_sb%d" % h) for h in range(2)]
+        dlT = keep.tile([P, 4, P], BF16, name="dlT")
+
+        def x_turn(g, tag):
+            xw = x_sb[g][:].bitcast(F32)
+            xgw = x_grp[g][:].bitcast(F32)
+            for hh in range(2):
+                xt = ps.tile([P, 4, P], F32, name="xt", tag=tag, bufs=2)
+                for j in range(4):
+                    px, u = hh * 2 + j // 2, j % 2
+                    nc.tensor.transpose(
+                        xt[:, j, :], xw[:, px * 256 + u : (px + 1) * 256 : 2], ident_f[:]
+                    )
+                nc.scalar.copy(
+                    out=xgw[:, hh * 512 : (hh + 1) * 512].rearrange(
+                        "p (h b u) -> p h b u", h=2, u=2
+                    ),
+                    in_=xt[:].rearrange("p (h u) b -> p h b u", h=2),
+                )
+
+        def x_quant(g):
+            nc.vector.quantize_mx(
+                out=x_codes[g][:].bitcast(FP8X4), scales=x_scales[g][:], in_=x_grp[g][:]
+            )
+
+        def mx(s, times=1):
+            ct, g = s // NG, s % NG
+            acc = ps.tile([P, 512], F32, name="acc", tag="p", bufs=2)
+            for rep in range(times):
+                nc.tensor.matmul_mx(
+                    out=acc[:],
+                    lhsT=w_codes[:, ct * P : (ct + 1) * P].bitcast(FP8X4),
+                    lhsT_scale=w_scales[:, ct * P : (ct + 1) * P],
+                    rhs=x_codes[g][:].bitcast(FP8X4),
+                    rhs_scale=x_scales[g][:],
+                    start=True,
+                    stop=True,
+                )
+            acc_t[s] = acc
+
+        def z_only(s):
+            z = work.tile([P, 512], F32, name="z", tag="z")
+            nc.vector.tensor_tensor(out=z[:], in0=acc_t[s][:], in1=t_add[s][:], op=ALU.add)
+            z_t[s] = z
+
+        def y_only(s):
+            z = z_t[s]
+            yt = keep.tile([P, 512], F32, name="y%d" % s)
+            nc.vector.scalar_tensor_tensor(
+                out=yt[:], in0=z[:], scalar=SLOPE, in1=z[:], op0=ALU.mult, op1=ALU.max
+            )
+            y_t[s] = yt
+
+        def square(s):
+            qt = work.tile([P, 512], F32, name="qt", tag="q")
+            nc.scalar.activation(out=qt[:], in_=y_t[s][:], func=ACT.Square)
+            q_t[s] = qt
+
+        def sums(s, k):
+            ct, g = s // NG, s % NG
+            if g == 0:
+                acc_sum = ps.tile([P, P], F32, name="acc_sum", tag=("sy" if k == 0 else "sq"))
+                sum_t[(ct, k)] = acc_sum
+            if True:
+                src = y_t[s] if k == 0 else q_t[s]
+                for j in range(4):
+                    hw = g * 4 + j
+                    nc.tensor.matmul(
+                        out=sum_t[(ct, k)][:],
+                        lhsT=src[:, j * P : (j + 1) * P],
+                        rhs=ident_f[:],
+                        is_transpose=True,
+                        start=(hw == 0),
+                        stop=(hw == HW - 1),
+                    )
+
+        def stats_a(ct):
+            mean = small.tile([P, P], F32, name="mean", tag="mean")
+            nc.scalar.activation(out=mean[:], in_=sum_t[(ct, 0)][:], func=ACT.Copy, scale=1.0 / HW)
+            msq = small.tile([P, P], F32, name="msq", tag="msq")
+            nc.scalar.activation(out=msq[:], in_=sum_t[(ct, 0)][:], func=ACT.Square, scale=1.0 / HW)
+            sm[("msq", ct)] = msq
+            sm[("mean", ct)] = mean
+
+        def stats_b(ct):
+            var = small.tile([P, P], F32, name="var", tag="var")
+            nc.vector.scalar_tensor_tensor(
+                out=var[:], in0=sum_t[(ct, 1)][:], scalar=1.0 / HW, in1=sm[("msq", ct)][:],
+                op0=ALU.mult, op1=ALU.subtract,
+            )
+            rstd = small.tile([P, P], F32, name="rstd", tag="rstd")
+            nc.scalar.activation(
+                out=rstd[:], in_=var[:], func=ACT.Abs_reciprocal_sqrt, bias=eps_t[:], scale=1.0
+            )
+            sm[("rstd", ct)] = rstd
+
+        def stats_c(ct):
+            cs = slice(ct * P, (ct + 1) * P)
+            rstd = sm[("rstd", ct)]
+            a_c = small.tile([P, P], F32, name="a_c", tag="a_c")
+            nc.vector.tensor_tensor(out=a_c[:], in0=rstd[:], in1=gb_sb[0][:, cs], op=ALU.mult)
+            sm[("ac", ct)] = a_c
+            m_a = small.tile([P, P], F32, name="m_a", tag="m_a")
+            nc.gpsimd.tensor_tensor(out=m_a[:], in0=sm[("mean", ct)][:], in1=a_c[:], op=ALU.mult)
+            b_c = small.tile([P, P], F32, name="b_c", tag="b_c", bufs=3)
+            nc.gpsimd.tensor_tensor(out=b_c[:], in0=gb_sb[1][:, cs], in1=m_a[:], op=ALU.subtract)
+            sm[("b", ct)] = b_c
+
+        def stats_d(ct):
+            a_ps = ps.tile([P, P], F32, name="a_ps", tag="a", bufs=2)
+            nc.tensor.transpose(a_ps[:], sm[("ac", ct)][:], ident_f[:])
+            sm[("a", ct)] = a_ps
+
+        def scale_y(e):
+            ct = e // NG
+            wt = work.tile([P, 4, P], F32, name="wt", tag="w", bufs=4)
+            nc.vector.tensor_tensor(
+                out=wt[:],
+                in0=y_t[e][:].rearrange("p (h b) -> p h b", h=4),
+                in1=sm[("a", ct)][:].unsqueeze(1).to_broadcast([P, 4, P]),
+                op=ALU.mult,
+            )
+            w_t[e] = wt
+
+        def turn_out(e, tag="o"):
+            o_ps = ps.tile([P, 4, P], F32, name="o_ps", tag=tag, bufs=2)
+            for j in range(4):
+                nc.tensor.transpose(o_ps[:, j, :], w_t[e][:, j, :], ident_f[:])
+            sm[("o", e)] = o_ps
+
+        def shift_store(e):
+            ct, g = e // NG, e % NG
+            ot = work.tile([P, 4, P], F32, name="ot", tag="ot", bufs=8)
+            nc.vector.tensor_tensor(
+                out=ot[:],
+                in0=sm[("o", e)][:],
+                in1=sm[("b", ct)][:].unsqueeze(1).to_broadcast([P, 4, P]),
+                op=ALU.add,
+            )
+            nc.sync.dma_start(out=outv[:, g * 4 : (g + 1) * 4, ct * P : (ct + 1) * P], in_=ot[:])
+
+        def shift_store_sg(e):
+            ct, g = e // NG, e % NG
+            ev = work.tile([P, 4, P], F32, name="ev", tag="ev")
+            nc.scalar.copy(out=ev[:], in_=sm[("o", e)][:])
+            ot = work.tile([P, 4, P], F32, name="ot", tag="ot", bufs=8)
+            nc.gpsimd.tensor_tensor(
+                out=ot[:],
+                in0=ev[:],
+                in1=sm[("b", ct)][:].unsqueeze(1).to_broadcast([P, 4, P]),
+                op=ALU.add,
+            )
+            nc.sync.dma_start(out=outv[:, g * 4 : (g + 1) * 4, ct * P : (ct + 1) * P], in_=ot[:])
+
+        def shift(e):
+            if e < 12 and e % 2 == 1 and USE_SG:
+                shift_store_sg(e)
+            else:
+                shift_store(e)
+
+        def style_turn():
+            dlT_ps = ps.tile([P, 4, P], BF16, name="dlT_ps", tag="a", bufs=2)
+            for kc in range(4):
+                nc.tensor.transpose(dlT_ps[:, kc, :], dl_sb[:, kc * P : (kc + 1) * P], ident_b[:])
+            nc.vector.tensor_copy(out=dlT[:], in_=dlT_ps[:])
+
+        def style_mm(half):
+            gb_ps = ps.tile([P, 512], F32, name="gb_ps", tag="o", bufs=2)
+            for kc in range(4):
+                nc.tensor.matmul(
+                    out=gb_ps[:],
+                    lhsT=dlT[:, kc, :],
+                    rhs=dw_sb[:, kc, half * 512 : (half + 1) * 512],
+                    start=(kc == 0),
+                    stop=(kc == 3),
+                )
+            sm[("gb", half)] = gb_ps
+
+        def style_out(half):
+            nc.vector.scalar_tensor_tensor(
+                out=gb_sb[half][:], in0=sm[("gb", half)][:], scalar=(1.0 if half == 0 else 0.0),
+                in1=db_bc[:, half * 512 : (half + 1) * 512], op0=ALU.add, op1=ALU.add,
+            )
+
+        noise_half(0)
+        x_turn(0, "o")
+        noise_half(1)
+        for s in range(NG):
+            noise_term(s)
+        w_quant()
+        x_turn(1, "p")
+        x_quant(0)
+        x_turn(2, "o")
+        mx(0)
+        x_quant(1)
+        x_turn(3, "o")
+        mx(1)
+        for i in range(NSTEP):
+            rel = [(ct, i - (NG * ct + NG - 1)) for ct in range(NCT)]
+            for ct, r in rel:
+                if r == 2:
+                    stats_a(ct)
+            if i - LAG - 2 >= 0:
+                shift(i - LAG - 2)
+            if i == 6:
+                style_out(0)
+                style_out(1)
+            for ct, r in rel:
+                if r == 3:
+                    stats_b(ct)
+            for ct, r in rel:
+                if r == 4:
+                    stats_c(ct)
+            if i - LAG - 1 >= 0:
+                turn_out(i - LAG - 1)
+            if i >= 2:
+                sums(i - 2, 1)
+            z_only(i)
+            if i + 2 < NG:
+                x_quant(i + 2)
+            if i - LAG >= 0:
+                scale_y(i - LAG)
+            y_only(i)
+            if i >= 1:
+                sums(i - 1, 0)
+            for ct, r in rel:
+                if r == 4:
+                    stats_d(ct)
+            if i + 2 < NSTEP:
+                mx(i + 2)
+            if i + NG < NSTEP:
+                noise_term_s(i + NG)
+            square(i)
+            if i == 3:
+                style_turn()
+            if i == 4:
+                style_mm(0)
+                style_mm(1)
+        last = NCT - 1
+        sums(NSTEP - 1, 0)
+        sums(NSTEP - 2, 1)
+        stats_a(last)
+        shift(6)
+        scale_y(8)
+        turn_out(7, "o")
+        sums(NSTEP - 1, 1)
+        shift(7)
+        scale_y(9)
+        turn_out(8, "p")
+        stats_b(last)
+        shift(8)
+        scale_y(10)
+        turn_out(9, "p")
+        shift(9)
+        scale_y(11)
+        turn_out(10, "o")
+        stats_c(last)
+        stats_d(last)
+        shift(10)
+        turn_out(11, "o")
+        shift(11)
+        for k in range(NG):
+            scale_y(12 + k)
+            turn_out(12 + k, "p" if k < 2 else "o")
+        for k in range(NG):
+            shift(12 + k)

@@ -20,9 +20,19 @@ NG = 4
 NCT = 4
 NSTEP = NG * NCT
 EPS = 1e-8
-SLOPE = 0.2
 LAG = 8
-USE_SG = True
+
+
+def exit_on_vector(e):
+    return e % 2 == 0
+
+
+def shift_on_gpsimd(e):
+    return False
+
+
+def y_on_vector(s):
+    return s % NG == NG - 1
 
 
 def tile_styleganlayerepilogue_kernel(
@@ -35,8 +45,31 @@ def tile_styleganlayerepilogue_kernel(
         small = ctx.enter_context(tc.tile_pool(name="small", bufs=2))
         ps = ctx.enter_context(tc.psum_pool(name="ps", bufs=1))
 
+        xv = x.rearrange("b h w c -> b (h w c)")
+        x_sb = [keep.tile([P, 2048], BF16, name="x_sb%d" % g) for g in range(NG)]
+        w_raw = keep.tile([P, 4, 512], BF16, name="w_raw")
+        nm_sb = keep.tile([P, HW], BF16, name="nm_sb")
+        dl_sb = keep.tile([P, 512], BF16, name="dl_sb")
+        dw_sb = keep.tile([P, 4, 1024], BF16, name="dw_sb")
+        db_bc = keep.tile([P, 1024], BF16, name="db_bc")
         rows = keep.tile([P, P], BF16, name="rows")
         nc.vector.memset(rows[:].bitcast(I32), 0)
+
+        nc.sync.dma_start(out=nm_sb[:], in_=noise_map.rearrange("b h w o -> b (h w o)"))
+        for half in range(2):
+            cs = slice(half * 1024, (half + 1) * 1024)
+            nc.sync.dma_start(out=x_sb[0][:, cs], in_=xv[:, cs])
+        nc.sync.dma_start(
+            out=rows[0:4, :], in_=noise_weight.rearrange("a b c (r n) -> (a b c r) n", r=4)
+        )
+        nc.sync.dma_start(out=rows[4:8, :], in_=bias.rearrange("a b c (r n) -> (a b c r) n", r=4))
+        nc.sync.dma_start(out=w_raw[:], in_=conv_w.rearrange("(p j) c -> p j c", j=4))
+        for g in (1, 2, 3):
+            nc.sync.dma_start(out=x_sb[g][:], in_=xv[:, g * 2048 : (g + 1) * 2048])
+        nc.sync.dma_start(out=dl_sb[:], in_=dlatents)
+        nc.sync.dma_start(out=dw_sb[:], in_=dense_w.rearrange("(k p) n -> p k n", p=P))
+        nc.sync.dma_start(out=db_bc[:], in_=dense_b.partition_broadcast(P))
+
         warm = keep.tile([P, 1], F32, name="warm")
         nc.vector.memset(warm[:], 1.0)
         ident_b = keep.tile([P, P], BF16, name="ident_b")
@@ -45,44 +78,25 @@ def tile_styleganlayerepilogue_kernel(
         make_identity(nc, ident_f[:])
         warm2 = keep.tile([P, 1], F32, name="warm2")
         eps_t = keep.tile([P, 1], F32, name="eps_t")
-        nc.vector.memset(eps_t[:], EPS)
-
-        xv = x.rearrange("b h w c -> b (h w c)")
-        x_sb = [keep.tile([P, 2048], BF16, name="x_sb%d" % g) for g in range(NG)]
-        w_raw = keep.tile([P, 4, 512], BF16, name="w_raw")
-        nm_sb = keep.tile([P, HW], BF16, name="nm_sb")
-        dl_sb = keep.tile([P, 512], BF16, name="dl_sb")
-        dw_sb = keep.tile([P, 4, 1024], BF16, name="dw_sb")
-
-        nc.sync.dma_start(out=nm_sb[:], in_=noise_map.rearrange("b h w o -> b (h w o)"))
-        nc.sync.dma_start(
-            out=rows[0:4, :], in_=noise_weight.rearrange("a b c (r n) -> (a b c r) n", r=4)
-        )
-        nc.sync.dma_start(out=rows[4:8, :], in_=bias.rearrange("a b c (r n) -> (a b c r) n", r=4))
+        nc.vector.memset(eps_t[:], 25.0 * EPS)
         nc.scalar.activation(out=warm2[:], in_=warm[:], func=ACT.Abs_reciprocal_sqrt)
-        nc.sync.dma_start(out=x_sb[0][:], in_=xv[:, 0:2048])
-        nc.sync.dma_start(
-            out=w_raw[:],
-            in_=conv_w.rearrange("(p j) c -> p j c", j=4),
-        )
-        for g in range(1, NG):
-            nc.sync.dma_start(out=x_sb[g][:], in_=xv[:, g * 2048 : (g + 1) * 2048])
-        nc.sync.dma_start(out=dl_sb[:], in_=dlatents)
-        nc.sync.dma_start(out=dw_sb[:], in_=dense_w.rearrange("(k p) n -> p k n", p=P))
-        db_bc = keep.tile([P, 1024], BF16, name="db_bc")
-        nc.sync.dma_start(out=db_bc[:], in_=dense_b.partition_broadcast(P))
 
-        cols_ps = ps.tile([P, P], BF16, name="cols_ps", tag="a", bufs=2)
-        nc.tensor.transpose(cols_ps[:], rows[:], ident_b[:])
-        cols = keep.tile([P, 8], F32, name="cols")
-        nc.vector.tensor_copy(out=cols[:], in_=cols_ps[:, 0:8])
-
-
+        nw_col = keep.tile([P, NCT], F32, name="nw_col")
+        b4_col = keep.tile([P, NCT], F32, name="b4_col")
         nm_bc = [keep.tile([P, 1024], BF16, name="nm_bc%d" % h) for h in range(2)]
-        t_add = {}
+
+        nm_t = {}
+
+        def columns():
+            cols_ps = ps.tile([P, P], BF16, name="cols_ps", tag="p", bufs=2)
+            nc.tensor.transpose(cols_ps[:], rows[:], ident_b[:])
+            nc.vector.tensor_copy(out=nw_col[:], in_=cols_ps[:, 0:4])
+            nc.vector.tensor_scalar(
+                out=b4_col[:], in0=cols_ps[:, 4:8], scalar1=4.0, scalar2=None, op0=ALU.mult
+            )
 
         def noise_half(half):
-            nm_ps = ps.tile([P, 1024], BF16, name="nm_ps%d" % half, tag=("sy" if half == 0 else "sq"))
+            nm_ps = ps.tile([P, 1024], BF16, name="nm_ps%d" % half, tag="ab", bufs=2)
             for j in range(8):
                 hw = half * 8 + j
                 nc.tensor.matmul(
@@ -92,109 +106,117 @@ def tile_styleganlayerepilogue_kernel(
                     start=True,
                     stop=True,
                 )
-            nc.scalar.copy(out=nm_bc[half][:], in_=nm_ps[:])
+            nm_t[half] = nm_ps
 
-        def noise_term(s):
-            ct, g = s // NG, s % NG
-            t_add[s] = keep.tile([P, 512], F32, name="t_add%d" % s)
-            nc.gpsimd.tensor_scalar(
-                out=t_add[s][:],
-                in0=nm_bc[g // 2][:, (g % 2) * 512 : (g % 2 + 1) * 512],
-                scalar1=cols[:, ct : ct + 1],
-                scalar2=cols[:, 4 + ct : 5 + ct],
-                op0=ALU.mult,
-                op1=ALU.add,
-            )
-
-        def noise_term_s(s):
-            ct, g = s // NG, s % NG
-            t_add[s] = keep.tile([P, 512], F32, name="t_add%d" % s)
-            nc.scalar.activation(
-                out=t_add[s][:],
-                in_=nm_bc[g // 2][:, (g % 2) * 512 : (g % 2 + 1) * 512],
-                func=ACT.Identity,
-                bias=cols[:, 4 + ct : 5 + ct],
-                scale=cols[:, ct : ct + 1],
-            )
+        def noise_copy(half):
+            nc.vector.tensor_copy(out=nm_bc[half][:], in_=nm_t[half][:])
 
         w_grp = keep.tile([P, 512, 4], BF16, name="w_grp", align_bytes=64)
         w_codes = keep.tile([P, 512], U32, name="w_codes", align_bytes=64)
         w_scales = keep.tile([P, 512], U8, name="w_scales", align_bytes=64)
 
-        def w_quant():
-            nc.vector.tensor_copy(out=w_grp[:], in_=w_raw[:].rearrange("p t c -> p c t"))
+        def w_group(lo, hi):
+            dst = w_grp[:, lo:hi, :]
+            src = w_raw[:, :, lo:hi].rearrange("p t c -> p c t")
+            if lo == 0:
+                nc.vector.tensor_copy(out=dst, in_=src)
+            else:
+                nc.gpsimd.tensor_scalar(
+                    out=dst, in0=src, scalar1=1.0, scalar2=0.0, op0=ALU.mult, op1=ALU.add
+                )
+
+        def w_quant(lo, hi):
             nc.vector.quantize_mx(
-                out=w_codes[:].bitcast(FP8X4),
-                scales=w_scales[:],
-                in_=w_grp[:].rearrange("p c t -> p (c t)"),
+                out=w_codes[:, lo:hi].bitcast(FP8X4),
+                scales=w_scales[:, lo:hi],
+                in_=w_grp[:, lo:hi, :].rearrange("p c t -> p (c t)"),
             )
 
         x_grp = [keep.tile([P, 2048], BF16, name="x_grp%d" % g, align_bytes=64) for g in range(NG)]
         x_codes = [keep.tile([P, 512], U32, name="x_codes%d" % g, align_bytes=64) for g in range(NG)]
         x_scales = [keep.tile([P, 512], U8, name="x_scales%d" % g, align_bytes=64) for g in range(NG)]
         outv = out.rearrange("b h w c -> b (h w) c")
+        xt_t = {}
         acc_t = {}
         z_t = {}
+        r_t = {}
         y_t = {}
         q_t = {}
         w_t = {}
+        o_t = {}
         sum_t = {}
-        st_t = {}
         sm = {}
         gb_sb = [keep.tile([P, 512], F32, name="gb_sb%d" % h) for h in range(2)]
         dlT = keep.tile([P, 4, P], BF16, name="dlT")
 
-        def x_turn(g, tag):
+        def x_turn(g, tags):
             xw = x_sb[g][:].bitcast(F32)
-            xgw = x_grp[g][:].bitcast(F32)
             for hh in range(2):
-                xt = ps.tile([P, 4, P], F32, name="xt", tag=tag, bufs=2)
+                tag = tags[hh]
+                xt = ps.tile([P, 4, P], F32, name="xt", tag=tag, bufs=(1 if tag[0] == "s" else 2))
                 for j in range(4):
                     px, u = hh * 2 + j // 2, j % 2
                     nc.tensor.transpose(
                         xt[:, j, :], xw[:, px * 256 + u : (px + 1) * 256 : 2], ident_f[:]
                     )
-                nc.scalar.copy(
-                    out=xgw[:, hh * 512 : (hh + 1) * 512].rearrange(
-                        "p (h b u) -> p h b u", h=2, u=2
-                    ),
-                    in_=xt[:].rearrange("p (h u) b -> p h b u", h=2),
-                )
+                xt_t[(g, hh)] = xt
+
+        def x_copy(g, hh, eng):
+            xgw = x_grp[g][:].bitcast(F32)
+            dst = xgw[:, hh * 512 : (hh + 1) * 512].rearrange("p (h b u) -> p h b u", h=2, u=2)
+            src = xt_t[(g, hh)][:].rearrange("p (h u) b -> p h b u", h=2)
+            if eng == "s":
+                nc.scalar.copy(out=dst, in_=src)
+            else:
+                nc.vector.tensor_copy(out=dst, in_=src)
 
         def x_quant(g):
             nc.vector.quantize_mx(
                 out=x_codes[g][:].bitcast(FP8X4), scales=x_scales[g][:], in_=x_grp[g][:]
             )
 
-        def mx(s, times=1):
+        def mx(s):
             ct, g = s // NG, s % NG
             acc = ps.tile([P, 512], F32, name="acc", tag="p", bufs=2)
-            for rep in range(times):
-                nc.tensor.matmul_mx(
-                    out=acc[:],
-                    lhsT=w_codes[:, ct * P : (ct + 1) * P].bitcast(FP8X4),
-                    lhsT_scale=w_scales[:, ct * P : (ct + 1) * P],
-                    rhs=x_codes[g][:].bitcast(FP8X4),
-                    rhs_scale=x_scales[g][:],
-                    start=True,
-                    stop=True,
-                )
+            nc.tensor.matmul_mx(
+                out=acc[:],
+                lhsT=w_codes[:, ct * P : (ct + 1) * P].bitcast(FP8X4),
+                lhsT_scale=w_scales[:, ct * P : (ct + 1) * P],
+                rhs=x_codes[g][:].bitcast(FP8X4),
+                rhs_scale=x_scales[g][:],
+                start=True,
+                stop=True,
+            )
             acc_t[s] = acc
 
-        def z_only(s):
+        def z_step(s):
+            ct, g = s // NG, s % NG
             z = work.tile([P, 512], F32, name="z", tag="z")
-            nc.vector.tensor_tensor(out=z[:], in0=acc_t[s][:], in1=t_add[s][:], op=ALU.add)
+            nc.vector.scalar_tensor_tensor(
+                out=z[:],
+                in0=nm_bc[g // 2][:, (g % 2) * 512 : (g % 2 + 1) * 512],
+                scalar=nw_col[:, ct : ct + 1],
+                in1=acc_t[s][:],
+                op0=ALU.mult,
+                op1=ALU.add,
+            )
             z_t[s] = z
 
-        def y_only(s):
-            z = z_t[s]
-            yt = keep.tile([P, 512], F32, name="y%d" % s)
-            nc.vector.scalar_tensor_tensor(
-                out=yt[:], in0=z[:], scalar=SLOPE, in1=z[:], op0=ALU.mult, op1=ALU.max
+        def r_step(s):
+            ct = s // NG
+            r = work.tile([P, 512], F32, name="r", tag="r")
+            nc.scalar.activation(
+                out=r[:], in_=z_t[s][:], func=ACT.Relu, bias=b4_col[:, ct : ct + 1], scale=4.0
             )
+            r_t[s] = r
+
+        def y_step(s):
+            yt = keep.tile([P, 512], F32, name="y%d" % s)
+            eng = nc.vector if y_on_vector(s) else nc.gpsimd
+            eng.tensor_tensor(out=yt[:], in0=z_t[s][:], in1=r_t[s][:], op=ALU.add)
             y_t[s] = yt
 
-        def square(s):
+        def q_step(s):
             qt = work.tile([P, 512], F32, name="qt", tag="q")
             nc.scalar.activation(out=qt[:], in_=y_t[s][:], func=ACT.Square)
             q_t[s] = qt
@@ -202,122 +224,147 @@ def tile_styleganlayerepilogue_kernel(
         def sums(s, k):
             ct, g = s // NG, s % NG
             if g == 0:
-                acc_sum = ps.tile([P, P], F32, name="acc_sum", tag=("sy" if k == 0 else "sq"))
-                sum_t[(ct, k)] = acc_sum
-            if True:
-                src = y_t[s] if k == 0 else q_t[s]
-                for j in range(4):
-                    hw = g * 4 + j
-                    nc.tensor.matmul(
-                        out=sum_t[(ct, k)][:],
-                        lhsT=src[:, j * P : (j + 1) * P],
-                        rhs=ident_f[:],
-                        is_transpose=True,
-                        start=(hw == 0),
-                        stop=(hw == HW - 1),
-                    )
+                sum_t[(ct, k)] = ps.tile([P, P], F32, name="acc_sum", tag=("sy" if k == 0 else "sq"))
+            src = y_t[s] if k == 0 else q_t[s]
+            for j in range(4):
+                hw = g * 4 + j
+                nc.tensor.matmul(
+                    out=sum_t[(ct, k)][:],
+                    lhsT=src[:, j * P : (j + 1) * P],
+                    rhs=ident_f[:],
+                    is_transpose=True,
+                    start=(hw == 0),
+                    stop=(hw == HW - 1),
+                )
 
-        def stats_a(ct):
+        def stats_m(ct):
             mean = small.tile([P, P], F32, name="mean", tag="mean")
-            nc.scalar.activation(out=mean[:], in_=sum_t[(ct, 0)][:], func=ACT.Copy, scale=1.0 / HW)
+            nc.scalar.activation(
+                out=mean[:], in_=sum_t[(ct, 0)][:], func=ACT.Copy, scale=1.0 / HW
+            )
             msq = small.tile([P, P], F32, name="msq", tag="msq")
-            nc.scalar.activation(out=msq[:], in_=sum_t[(ct, 0)][:], func=ACT.Square, scale=1.0 / HW)
-            sm[("msq", ct)] = msq
+            nc.scalar.activation(out=msq[:], in_=sum_t[(ct, 0)][:], func=ACT.Square)
             sm[("mean", ct)] = mean
+            sm[("msq", ct)] = msq
 
-        def stats_b(ct):
+        def stats_var(ct):
             var = small.tile([P, P], F32, name="var", tag="var")
             nc.vector.scalar_tensor_tensor(
-                out=var[:], in0=sum_t[(ct, 1)][:], scalar=1.0 / HW, in1=sm[("msq", ct)][:],
+                out=var[:], in0=sum_t[(ct, 1)][:], scalar=float(HW), in1=sm[("msq", ct)][:],
                 op0=ALU.mult, op1=ALU.subtract,
             )
+            sm[("var", ct)] = var
+
+        def stats_rstd(ct):
             rstd = small.tile([P, P], F32, name="rstd", tag="rstd")
             nc.scalar.activation(
-                out=rstd[:], in_=var[:], func=ACT.Abs_reciprocal_sqrt, bias=eps_t[:], scale=1.0
+                out=rstd[:], in_=sm[("var", ct)][:], func=ACT.Abs_reciprocal_sqrt, bias=eps_t[:],
+                scale=1.0 / (HW * HW),
             )
             sm[("rstd", ct)] = rstd
 
-        def stats_c(ct):
+        def stats_a(ct):
             cs = slice(ct * P, (ct + 1) * P)
-            rstd = sm[("rstd", ct)]
-            a_c = small.tile([P, P], F32, name="a_c", tag="a_c")
-            nc.vector.tensor_tensor(out=a_c[:], in0=rstd[:], in1=gb_sb[0][:, cs], op=ALU.mult)
-            sm[("ac", ct)] = a_c
-            m_a = small.tile([P, P], F32, name="m_a", tag="m_a")
-            nc.gpsimd.tensor_tensor(out=m_a[:], in0=sm[("mean", ct)][:], in1=a_c[:], op=ALU.mult)
-            b_c = small.tile([P, P], F32, name="b_c", tag="b_c", bufs=3)
-            nc.gpsimd.tensor_tensor(out=b_c[:], in0=gb_sb[1][:, cs], in1=m_a[:], op=ALU.subtract)
-            sm[("b", ct)] = b_c
+            a = small.tile([P, P], F32, name="a", tag="a")
+            nc.vector.tensor_tensor(out=a[:], in0=sm[("rstd", ct)][:], in1=gb_sb[0][:, cs], op=ALU.mult)
+            sm[("a", ct)] = a
 
-        def stats_d(ct):
-            a_ps = ps.tile([P, P], F32, name="a_ps", tag="a", bufs=2)
-            nc.tensor.transpose(a_ps[:], sm[("ac", ct)][:], ident_f[:])
-            sm[("a", ct)] = a_ps
+        def stats_b(ct):
+            cs = slice(ct * P, (ct + 1) * P)
+            eng = nc.gpsimd
+            ma = small.tile([P, P], F32, name="ma", tag="ma")
+            eng.tensor_tensor(out=ma[:], in0=sm[("mean", ct)][:], in1=sm[("a", ct)][:], op=ALU.mult)
+            b = small.tile([P, P], F32, name="b", tag="b")
+            eng.tensor_tensor(out=b[:], in0=gb_sb[1][:, cs], in1=ma[:], op=ALU.subtract)
+            sm[("b", ct)] = b
 
-        def scale_y(e):
+        def stats_ta(ct):
+            tag, bufs = ("sy", 1) if ct == NCT - 1 else ("ab", 2)
+            a_ps = ps.tile([P, P], F32, name="a_ps", tag=tag, bufs=bufs)
+            nc.tensor.transpose(a_ps[:], sm[("a", ct)][:], ident_f[:])
+            sm[("aT", ct)] = a_ps
+
+        def stats_tb(ct):
+            tag, bufs = ("sq", 1) if ct == NCT - 1 else ("ab", 2)
+            b_ps = ps.tile([P, P], F32, name="b_ps", tag=tag, bufs=bufs)
+            nc.tensor.transpose(b_ps[:], sm[("b", ct)][:], ident_f[:])
+            sm[("b_ps", ct)] = b_ps
+
+        def stats_bt(ct):
+            bT = small.tile([P, P], F32, name="bT", tag="bT")
+            nc.scalar.copy(out=bT[:], in_=sm[("b_ps", ct)][:])
+            sm[("bT", ct)] = bT
+
+        def w_step(e):
             ct = e // NG
             wt = work.tile([P, 4, P], F32, name="wt", tag="w", bufs=4)
             nc.vector.tensor_tensor(
                 out=wt[:],
                 in0=y_t[e][:].rearrange("p (h b) -> p h b", h=4),
-                in1=sm[("a", ct)][:].unsqueeze(1).to_broadcast([P, 4, P]),
+                in1=sm[("aT", ct)][:].unsqueeze(1).to_broadcast([P, 4, P]),
                 op=ALU.mult,
             )
             w_t[e] = wt
 
         def turn_out(e, tag="o"):
+            ct = e // NG
             o_ps = ps.tile([P, 4, P], F32, name="o_ps", tag=tag, bufs=2)
+            add_b = not exit_on_vector(e) and not shift_on_gpsimd(e)
             for j in range(4):
-                nc.tensor.transpose(o_ps[:, j, :], w_t[e][:, j, :], ident_f[:])
-            sm[("o", e)] = o_ps
+                nc.tensor.matmul(
+                    out=o_ps[:, j, :], lhsT=w_t[e][:, j, :], rhs=ident_f[:],
+                    is_transpose=True, start=True, stop=not add_b,
+                )
+                if add_b:
+                    nc.tensor.matmul(
+                        out=o_ps[:, j, :], lhsT=sm[("bT", ct)][:], rhs=ident_f[:],
+                        is_transpose=True, start=False, stop=True,
+                    )
+            o_t[e] = o_ps
 
-        def shift_store(e):
+        def exit_step(e):
             ct, g = e // NG, e % NG
-            ot = work.tile([P, 4, P], F32, name="ot", tag="ot", bufs=8)
-            nc.vector.tensor_tensor(
-                out=ot[:],
-                in0=sm[("o", e)][:],
-                in1=sm[("b", ct)][:].unsqueeze(1).to_broadcast([P, 4, P]),
-                op=ALU.add,
-            )
-            nc.sync.dma_start(out=outv[:, g * 4 : (g + 1) * 4, ct * P : (ct + 1) * P], in_=ot[:])
-
-        def shift_store_sg(e):
-            ct, g = e // NG, e % NG
-            ev = work.tile([P, 4, P], F32, name="ev", tag="ev")
-            nc.scalar.copy(out=ev[:], in_=sm[("o", e)][:])
-            ot = work.tile([P, 4, P], F32, name="ot", tag="ot", bufs=8)
-            nc.gpsimd.tensor_tensor(
-                out=ot[:],
-                in0=ev[:],
-                in1=sm[("b", ct)][:].unsqueeze(1).to_broadcast([P, 4, P]),
-                op=ALU.add,
-            )
-            nc.sync.dma_start(out=outv[:, g * 4 : (g + 1) * 4, ct * P : (ct + 1) * P], in_=ot[:])
-
-        def shift(e):
-            if e < 12 and e % 2 == 1 and USE_SG:
-                shift_store_sg(e)
+            ot = work.tile([P, 4, P], F32, name="ot", tag="ot", bufs=6)
+            if exit_on_vector(e):
+                nc.vector.tensor_tensor(
+                    out=ot[:],
+                    in0=o_t[e][:],
+                    in1=sm[("b", ct)][:].unsqueeze(1).to_broadcast([P, 4, P]),
+                    op=ALU.add,
+                )
+            elif shift_on_gpsimd(e):
+                ev = work.tile([P, 4, P], F32, name="ev", tag="ev")
+                nc.scalar.copy(out=ev[:], in_=o_t[e][:])
+                nc.gpsimd.tensor_tensor(
+                    out=ot[:],
+                    in0=ev[:],
+                    in1=sm[("b", ct)][:].unsqueeze(1).to_broadcast([P, 4, P]),
+                    op=ALU.add,
+                )
             else:
-                shift_store(e)
+                nc.scalar.copy(out=ot[:], in_=o_t[e][:])
+            nc.sync.dma_start(out=outv[:, g * 4 : (g + 1) * 4, ct * P : (ct + 1) * P], in_=ot[:])
 
         def style_turn():
-            dlT_ps = ps.tile([P, 4, P], BF16, name="dlT_ps", tag="a", bufs=2)
+            dlT_ps = ps.tile([P, 4, P], BF16, name="dlT_ps", tag="ab", bufs=2)
             for kc in range(4):
                 nc.tensor.transpose(dlT_ps[:, kc, :], dl_sb[:, kc * P : (kc + 1) * P], ident_b[:])
-            nc.vector.tensor_copy(out=dlT[:], in_=dlT_ps[:])
+            sm["dlT_ps"] = dlT_ps
 
-        def style_mm(half):
-            gb_ps = ps.tile([P, 512], F32, name="gb_ps", tag="o", bufs=2)
-            for kc in range(4):
-                nc.tensor.matmul(
-                    out=gb_ps[:],
-                    lhsT=dlT[:, kc, :],
-                    rhs=dw_sb[:, kc, half * 512 : (half + 1) * 512],
-                    start=(kc == 0),
-                    stop=(kc == 3),
-                )
-            sm[("gb", half)] = gb_ps
+        def style_copy():
+            nc.vector.tensor_copy(out=dlT[:], in_=sm["dlT_ps"][:])
+
+        def style_mm(n):
+            half, kc = n // 4, n % 4
+            if kc == 0:
+                sm[("gb", half)] = ps.tile([P, 512], F32, name="gb_ps", tag="ab", bufs=2)
+            nc.tensor.matmul(
+                out=sm[("gb", half)][:],
+                lhsT=dlT[:, kc, :],
+                rhs=dw_sb[:, kc, half * 512 : (half + 1) * 512],
+                start=(kc == 0),
+                stop=(kc == 3),
+            )
 
         def style_out(half):
             nc.vector.scalar_tensor_tensor(
@@ -325,85 +372,92 @@ def tile_styleganlayerepilogue_kernel(
                 in1=db_bc[:, half * 512 : (half + 1) * 512], op0=ALU.add, op1=ALU.add,
             )
 
-        noise_half(0)
-        x_turn(0, "o")
-        noise_half(1)
-        for s in range(NG):
-            noise_term(s)
-        w_quant()
-        x_turn(1, "p")
+        ctx.enter_context(tc.manual_schedule())
+        x_turn(0, ("o", "o"))
+        x_copy(0, 0, "v")
+        x_copy(0, 1, "s")
+        w_group(0, P)
+        w_quant(0, P)
         x_quant(0)
-        x_turn(2, "o")
+        noise_half(0)
+        noise_copy(0)
+        columns()
+        x_turn(1, ("sy", "sq"))
         mx(0)
-        x_quant(1)
-        x_turn(3, "o")
-        mx(1)
-        for i in range(NSTEP):
-            rel = [(ct, i - (NG * ct + NG - 1)) for ct in range(NCT)]
-            for ct, r in rel:
-                if r == 2:
+        x_copy(1, 0, "s")
+        x_copy(1, 1, "s")
+        w_group(P, 4 * P)
+        x_turn(2, ("o", "o"))
+        noise_half(1)
+        for i in range(NSTEP + LAG + 2):
+            due = [(ct, i - (NG * ct + NG - 1)) for ct in range(NCT)]
+            conv = i < NSTEP
+            e_out = i - LAG - 2
+            if conv:
+                z_step(i)
+            for ct, k in due:
+                if k == 3:
+                    stats_var(ct)
+                if k == 4:
                     stats_a(ct)
-            if i - LAG - 2 >= 0:
-                shift(i - LAG - 2)
-            if i == 6:
-                style_out(0)
-                style_out(1)
-            for ct, r in rel:
-                if r == 3:
-                    stats_b(ct)
-            for ct, r in rel:
-                if r == 4:
-                    stats_c(ct)
-            if i - LAG - 1 >= 0:
-                turn_out(i - LAG - 1)
-            if i >= 2:
-                sums(i - 2, 1)
-            z_only(i)
-            if i + 2 < NG:
-                x_quant(i + 2)
-            if i - LAG >= 0:
-                scale_y(i - LAG)
-            y_only(i)
-            if i >= 1:
-                sums(i - 1, 0)
-            for ct, r in rel:
-                if r == 4:
-                    stats_d(ct)
-            if i + 2 < NSTEP:
-                mx(i + 2)
-            if i + NG < NSTEP:
-                noise_term_s(i + NG)
-            square(i)
-            if i == 3:
+            if i == 1:
+                style_copy()
+                for n in range(4):
+                    style_mm(n)
+            if i == 2:
+                for n in range(4, 8):
+                    style_mm(n)
+            if i < 3:
+                x_quant(i + 1)
+            if i + 1 < NSTEP:
+                mx(i + 1)
+            if i == 0:
+                noise_copy(1)
+                x_turn(3, ("sy", "sq"))
                 style_turn()
-            if i == 4:
-                style_mm(0)
-                style_mm(1)
-        last = NCT - 1
-        sums(NSTEP - 1, 0)
-        sums(NSTEP - 2, 1)
-        stats_a(last)
-        shift(6)
-        scale_y(8)
-        turn_out(7, "o")
-        sums(NSTEP - 1, 1)
-        shift(7)
-        scale_y(9)
-        turn_out(8, "p")
-        stats_b(last)
-        shift(8)
-        scale_y(10)
-        turn_out(9, "p")
-        shift(9)
-        scale_y(11)
-        turn_out(10, "o")
-        stats_c(last)
-        stats_d(last)
-        shift(10)
-        turn_out(11, "o")
-        shift(11)
-        for k in range(NG):
-            scale_y(12 + k)
-            turn_out(12 + k, "p" if k < 2 else "o")
-        for k in range(NG):
-            shift(12 + k)
+            if i == 1:
+                w_quant(P, 2 * P)
+                w_quant(2 * P, 4 * P)
+            if 1 <= i <= NSTEP:
+                y_step(i - 1)
+            for ct, k in due:
+                if k == 4:
+                    stats_b(ct)
+            if 2 <= i < NSTEP + 2 and (i - 2) % NG != NG - 1:
+                q_step(i - 2)
+            if e_out >= 0 and not exit_on_vector(e_out):
+                exit_step(e_out)
+            for ct, k in due:
+                if k == 3:
+                    stats_rstd(ct)
+            if conv:
+                r_step(i)
+            if 1 <= i <= NSTEP and (i - 1) % NG == NG - 1:
+                q_step(i - 1)
+            if i < 2:
+                x_copy(i + 2, 0, "s")
+                x_copy(i + 2, 1, "v" if i == 0 else "s")
+            if 2 <= i < NSTEP + 2:
+                sums(i - 2, 0)
+            if 3 <= i < NSTEP + 3 and (i - 3) % NG != NG - 1:
+                sums(i - 3, 1)
+            if 2 <= i < NSTEP + 2 and (i - 2) % NG == NG - 1:
+                sums(i - 2, 1)
+            for ct, k in due:
+                if k == 2:
+                    stats_m(ct)
+                if k == 6:
+                    stats_bt(ct)
+            if 0 <= i - LAG < NSTEP:
+                w_step(i - LAG)
+            if 0 <= i - LAG - 1 < NSTEP:
+                turn_out(i - LAG - 1, "o" if i < NSTEP or i % 2 == 0 else "p")
+            if e_out >= 0 and exit_on_vector(e_out):
+                exit_step(e_out)
+            for ct, k in due:
+                if k == 4:
+                    stats_ta(ct)
+                if k == 5:
+                    stats_tb(ct)
+            if i in (3, 4):
+                style_out(i - 3)

@@ -32,7 +32,7 @@ def shift_on_gpsimd(e):
 
 
 def y_on_vector(s):
-    return s % NG == NG - 1
+    return s < 3 or s % NG == NG - 1
 
 
 def tile_styleganlayerepilogue_kernel(
@@ -116,14 +116,9 @@ def tile_styleganlayerepilogue_kernel(
         w_scales = keep.tile([P, 512], U8, name="w_scales", align_bytes=64)
 
         def w_group(lo, hi):
-            dst = w_grp[:, lo:hi, :]
-            src = w_raw[:, :, lo:hi].rearrange("p t c -> p c t")
-            if lo == 0:
-                nc.vector.tensor_copy(out=dst, in_=src)
-            else:
-                nc.gpsimd.tensor_scalar(
-                    out=dst, in0=src, scalar1=1.0, scalar2=0.0, op0=ALU.mult, op1=ALU.add
-                )
+            nc.vector.tensor_copy(
+                out=w_grp[:, lo:hi, :], in_=w_raw[:, :, lo:hi].rearrange("p t c -> p c t")
+            )
 
         def w_quant(lo, hi):
             nc.vector.quantize_mx(
@@ -266,7 +261,7 @@ def tile_styleganlayerepilogue_kernel(
         def stats_a(ct):
             cs = slice(ct * P, (ct + 1) * P)
             a = small.tile([P, P], F32, name="a", tag="a")
-            nc.vector.tensor_tensor(out=a[:], in0=sm[("rstd", ct)][:], in1=gb_sb[0][:, cs], op=ALU.mult)
+            nc.gpsimd.tensor_tensor(out=a[:], in0=sm[("rstd", ct)][:], in1=gb_sb[0][:, cs], op=ALU.mult)
             sm[("a", ct)] = a
 
         def stats_b(ct):
@@ -386,7 +381,6 @@ def tile_styleganlayerepilogue_kernel(
         mx(0)
         x_copy(1, 0, "s")
         x_copy(1, 1, "s")
-        w_group(P, 4 * P)
         x_turn(2, ("o", "o"))
         noise_half(1)
         for i in range(NSTEP + LAG + 2):
@@ -415,9 +409,10 @@ def tile_styleganlayerepilogue_kernel(
                 noise_copy(1)
                 x_turn(3, ("sy", "sq"))
                 style_turn()
-            if i == 1:
-                w_quant(P, 2 * P)
-                w_quant(2 * P, 4 * P)
+            if i < 3:
+                w_group((i + 1) * P, (i + 2) * P)
+            if 1 <= i < 4:
+                w_quant(i * P, (i + 1) * P)
             if 1 <= i <= NSTEP:
                 y_step(i - 1)
             for ct, k in due:

@@ -24,7 +24,7 @@ LAG = 8
 
 
 def exit_on_vector(e):
-    return e % 2 == 0
+    return e%4==0 or e>12
 
 
 def shift_on_gpsimd(e):
@@ -32,7 +32,7 @@ def shift_on_gpsimd(e):
 
 
 def y_on_vector(s):
-    return s < 3 or s % NG == NG - 1
+    return s < 8 or s % NG == NG - 1
 
 
 def tile_styleganlayerepilogue_kernel(
@@ -51,7 +51,11 @@ def tile_styleganlayerepilogue_kernel(
         nm_sb = keep.tile([P, HW], BF16, name="nm_sb")
         dl_sb = keep.tile([P, 512], BF16, name="dl_sb")
         dw_sb = keep.tile([P, 4, 1024], BF16, name="dw_sb")
-        db_bc = keep.tile([P, 1024], BF16, name="db_bc")
+        db_row = keep.tile([P, 1024], BF16, name="db_row")
+        nc.gpsimd.memset(db_row[:], 0.0)
+        ones_row = keep.tile([P, P], BF16, name="ones_row")
+        nc.gpsimd.memset(ones_row[:], 0.0)
+        nc.gpsimd.memset(ones_row[0:1, :], 1.0)
         rows = keep.tile([P, P], BF16, name="rows")
         nc.vector.memset(rows[:].bitcast(I32), 0)
 
@@ -64,11 +68,12 @@ def tile_styleganlayerepilogue_kernel(
         )
         nc.sync.dma_start(out=rows[4:8, :], in_=bias.rearrange("a b c (r n) -> (a b c r) n", r=4))
         nc.sync.dma_start(out=w_raw[:], in_=conv_w.rearrange("(p j) c -> p j c", j=4))
-        for g in (1, 2, 3):
-            nc.sync.dma_start(out=x_sb[g][:], in_=xv[:, g * 2048 : (g + 1) * 2048])
+        nc.sync.dma_start(out=x_sb[1][:], in_=xv[:, 2048:4096])
         nc.sync.dma_start(out=dl_sb[:], in_=dlatents)
+        for g in (2, 3):
+            nc.sync.dma_start(out=x_sb[g][:], in_=xv[:, g * 2048 : (g + 1) * 2048])
         nc.sync.dma_start(out=dw_sb[:], in_=dense_w.rearrange("(k p) n -> p k n", p=P))
-        nc.sync.dma_start(out=db_bc[:], in_=dense_b.partition_broadcast(P))
+        nc.sync.dma_start(out=db_row[0:1, :], in_=dense_b.rearrange("(o n) -> o n", o=1))
 
         warm = keep.tile([P, 1], F32, name="warm")
         nc.vector.memset(warm[:], 1.0)
@@ -99,17 +104,18 @@ def tile_styleganlayerepilogue_kernel(
             nm_ps = ps.tile([P, 1024], BF16, name="nm_ps%d" % half, tag="ab", bufs=2)
             for j in range(8):
                 hw = half * 8 + j
-                nc.tensor.matmul(
-                    out=nm_ps[:, j * P : (j + 1) * P],
-                    lhsT=nm_sb[:, hw : hw + 1].to_broadcast([P, P]),
-                    rhs=ident_b[:],
-                    start=True,
-                    stop=True,
+                nc.tensor.transpose(
+                    nm_ps[:, j * P : (j + 1) * P],
+                    nm_sb[:, hw : hw + 1].to_broadcast([P, P]),
+                    ident_b[:],
                 )
             nm_t[half] = nm_ps
 
         def noise_copy(half):
-            nc.vector.tensor_copy(out=nm_bc[half][:], in_=nm_t[half][:])
+            if half == 0:
+                nc.vector.tensor_copy(out=nm_bc[half][:], in_=nm_t[half][:])
+            else:
+                nc.scalar.copy(out=nm_bc[half][:], in_=nm_t[half][:])
 
         w_grp = keep.tile([P, 512, 4], BF16, name="w_grp", align_bytes=64)
         w_codes = keep.tile([P, 512], U32, name="w_codes", align_bytes=64)
@@ -341,30 +347,33 @@ def tile_styleganlayerepilogue_kernel(
             nc.sync.dma_start(out=outv[:, g * 4 : (g + 1) * 4, ct * P : (ct + 1) * P], in_=ot[:])
 
         def style_turn():
-            dlT_ps = ps.tile([P, 4, P], BF16, name="dlT_ps", tag="ab", bufs=2)
+            dlT_ps = ps.tile([P, 4, P], BF16, name="dlT_ps", tag="p", bufs=2)
             for kc in range(4):
                 nc.tensor.transpose(dlT_ps[:, kc, :], dl_sb[:, kc * P : (kc + 1) * P], ident_b[:])
             sm["dlT_ps"] = dlT_ps
 
         def style_copy():
-            nc.vector.tensor_copy(out=dlT[:], in_=sm["dlT_ps"][:])
+            nc.scalar.copy(out=dlT[:], in_=sm["dlT_ps"][:])
 
         def style_mm(n):
             half, kc = n // 4, n % 4
+            cs = slice(half * 512, (half + 1) * 512)
             if kc == 0:
                 sm[("gb", half)] = ps.tile([P, 512], F32, name="gb_ps", tag="ab", bufs=2)
             nc.tensor.matmul(
-                out=sm[("gb", half)][:],
-                lhsT=dlT[:, kc, :],
-                rhs=dw_sb[:, kc, half * 512 : (half + 1) * 512],
-                start=(kc == 0),
-                stop=(kc == 3),
+                out=sm[("gb", half)][:], lhsT=dlT[:, kc, :], rhs=dw_sb[:, kc, cs],
+                start=(kc == 0), stop=False,
             )
+            if kc == 3:
+                nc.tensor.matmul(
+                    out=sm[("gb", half)][:], lhsT=ones_row[:], rhs=db_row[:, cs],
+                    start=False, stop=True,
+                )
 
         def style_out(half):
-            nc.vector.scalar_tensor_tensor(
-                out=gb_sb[half][:], in0=sm[("gb", half)][:], scalar=(1.0 if half == 0 else 0.0),
-                in1=db_bc[:, half * 512 : (half + 1) * 512], op0=ALU.add, op1=ALU.add,
+            nc.scalar.activation(
+                out=gb_sb[half][:], in_=sm[("gb", half)][:], func=ACT.Identity,
+                bias=(1.0 if half == 0 else 0.0), scale=1.0,
             )
 
         ctx.enter_context(tc.manual_schedule())
@@ -382,7 +391,10 @@ def tile_styleganlayerepilogue_kernel(
         x_copy(1, 0, "s")
         x_copy(1, 1, "s")
         x_turn(2, ("o", "o"))
+        x_copy(2, 0, "s")
         noise_half(1)
+        style_turn()
+        x_turn(3, ("sy", "sq"))
         for i in range(NSTEP + LAG + 2):
             due = [(ct, i - (NG * ct + NG - 1)) for ct in range(NCT)]
             conv = i < NSTEP
@@ -395,20 +407,18 @@ def tile_styleganlayerepilogue_kernel(
                 if k == 4:
                     stats_a(ct)
             if i == 1:
-                style_copy()
                 for n in range(4):
-                    style_mm(n)
-            if i == 2:
-                for n in range(4, 8):
                     style_mm(n)
             if i < 3:
                 x_quant(i + 1)
             if i + 1 < NSTEP:
                 mx(i + 1)
             if i == 0:
-                noise_copy(1)
-                x_turn(3, ("sy", "sq"))
-                style_turn()
+                x_copy(2, 1, "v")
+            if i == 1:
+                x_copy(3, 1, "s")
+                for n in range(4, 8):
+                    style_mm(n)
             if i < 3:
                 w_group((i + 1) * P, (i + 2) * P)
             if 1 <= i < 4:
@@ -427,11 +437,12 @@ def tile_styleganlayerepilogue_kernel(
                     stats_rstd(ct)
             if conv:
                 r_step(i)
+            if i == 0:
+                noise_copy(1)
+                style_copy()
+                x_copy(3, 0, "s")
             if 1 <= i <= NSTEP and (i - 1) % NG == NG - 1:
                 q_step(i - 1)
-            if i < 2:
-                x_copy(i + 2, 0, "s")
-                x_copy(i + 2, 1, "v" if i == 0 else "s")
             if 2 <= i < NSTEP + 2:
                 sums(i - 2, 0)
             if 3 <= i < NSTEP + 3 and (i - 3) % NG != NG - 1:
@@ -454,5 +465,5 @@ def tile_styleganlayerepilogue_kernel(
                     stats_ta(ct)
                 if k == 5:
                     stats_tb(ct)
-            if i in (3, 4):
-                style_out(i - 3)
+            if i in (1, 2):
+                style_out(i - 1)

@@ -239,12 +239,12 @@ def tile_styleganlayerepilogue_kernel(
                 )
 
         def stats_m(ct):
+            msq = small.tile([P, P], F32, name="msq", tag="msq")
+            nc.scalar.activation(out=msq[:], in_=sum_t[(ct, 0)][:], func=ACT.Square)
             mean = small.tile([P, P], F32, name="mean", tag="mean")
             nc.scalar.activation(
                 out=mean[:], in_=sum_t[(ct, 0)][:], func=ACT.Copy, scale=1.0 / HW
             )
-            msq = small.tile([P, P], F32, name="msq", tag="msq")
-            nc.scalar.activation(out=msq[:], in_=sum_t[(ct, 0)][:], func=ACT.Square)
             sm[("mean", ct)] = mean
             sm[("msq", ct)] = msq
 
@@ -393,8 +393,6 @@ def tile_styleganlayerepilogue_kernel(
         x_turn(2, ("o", "o"))
         x_copy(2, 0, "s")
         noise_half(1)
-        style_turn()
-        x_turn(3, ("sy", "sq"))
         for i in range(NSTEP + LAG + 2):
             due = [(ct, i - (NG * ct + NG - 1)) for ct in range(NCT)]
             conv = i < NSTEP
@@ -406,18 +404,18 @@ def tile_styleganlayerepilogue_kernel(
                     stats_var(ct)
                 if k == 4:
                     stats_a(ct)
-            if i == 1:
-                for n in range(4):
-                    style_mm(n)
             if i < 3:
                 x_quant(i + 1)
             if i + 1 < NSTEP:
                 mx(i + 1)
             if i == 0:
+                style_turn()
+                x_turn(3, ("sy", "sq"))
                 x_copy(2, 1, "v")
             if i == 1:
                 x_copy(3, 1, "s")
-                for n in range(4, 8):
+            if i in (1, 2):
+                for n in range(4 * i - 4, 4 * i):
                     style_mm(n)
             if i < 3:
                 w_group((i + 1) * P, (i + 2) * P)
@@ -465,5 +463,5 @@ def tile_styleganlayerepilogue_kernel(
                     stats_ta(ct)
                 if k == 5:
                     stats_tb(ct)
-            if i in (1, 2):
-                style_out(i - 1)
+            if i in (2, 3):
+                style_out(i - 2)

@@ -310,6 +310,16 @@ def tile_styleganlayerepilogue_kernel(
         def turn_out(e, tag="o"):
             ct = e // NG
             o_ps = ps.tile([P, 4, P], F32, name="o_ps", tag=tag, bufs=2)
+            if e >= 8 and e % 2 == 0:
+                nc.tensor.matmul_mx(
+                    out=o_ps[:].rearrange("p h c -> p (h c)"),
+                    lhsT=w_codes[:, 0:P].bitcast(FP8X4),
+                    lhsT_scale=w_scales[:, 0:P],
+                    rhs=x_codes[0][:].bitcast(FP8X4),
+                    rhs_scale=x_scales[0][:],
+                    start=True,
+                    stop=True,
+                )
             add_b = not exit_on_vector(e) and not shift_on_gpsimd(e)
             for j in range(4):
                 nc.tensor.matmul(

@@ -20,11 +20,12 @@ NG = 4
 NCT = 4
 NSTEP = NG * NCT
 EPS = 1e-8
-LAG = 8
+UNITS = list(range(NSTEP))
+STEP = [UNITS.index(u) for u in range(NSTEP)]
 
 
 def exit_on_vector(e):
-    return e%4==0 or e>12
+    return e % 2 == 0 or e > 12
 
 
 def shift_on_gpsimd(e):
@@ -47,7 +48,8 @@ def tile_styleganlayerepilogue_kernel(
 
         xv = x.rearrange("b h w c -> b (h w c)")
         x_sb = [keep.tile([P, 2048], BF16, name="x_sb%d" % g) for g in range(NG)]
-        w_raw = keep.tile([P, 4, 512], BF16, name="w_raw")
+        w_raw0 = keep.tile([P, 4, P], BF16, name="w_raw0")
+        w_raw1 = keep.tile([P, 4, 384], BF16, name="w_raw1")
         nm_sb = keep.tile([P, HW], BF16, name="nm_sb")
         dl_sb = keep.tile([P, 512], BF16, name="dl_sb")
         dw_sb = keep.tile([P, 4, 1024], BF16, name="dw_sb")
@@ -63,15 +65,17 @@ def tile_styleganlayerepilogue_kernel(
         for half in range(2):
             cs = slice(half * 1024, (half + 1) * 1024)
             nc.sync.dma_start(out=x_sb[0][:, cs], in_=xv[:, cs])
+        wv = conv_w.rearrange("(p j) c -> p j c", j=4)
+        nc.sync.dma_start(out=w_raw0[:], in_=wv[:, :, 0:P])
         nc.sync.dma_start(
             out=rows[0:4, :], in_=noise_weight.rearrange("a b c (r n) -> (a b c r) n", r=4)
         )
         nc.sync.dma_start(out=rows[4:8, :], in_=bias.rearrange("a b c (r n) -> (a b c r) n", r=4))
-        nc.sync.dma_start(out=w_raw[:], in_=conv_w.rearrange("(p j) c -> p j c", j=4))
         nc.sync.dma_start(out=x_sb[1][:], in_=xv[:, 2048:4096])
         nc.sync.dma_start(out=dl_sb[:], in_=dlatents)
-        for g in (2, 3):
-            nc.sync.dma_start(out=x_sb[g][:], in_=xv[:, g * 2048 : (g + 1) * 2048])
+        nc.sync.dma_start(out=x_sb[2][:], in_=xv[:, 4096:6144])
+        nc.sync.dma_start(out=w_raw1[:], in_=wv[:, :, P:512])
+        nc.sync.dma_start(out=x_sb[3][:], in_=xv[:, 6144:8192])
         nc.sync.dma_start(out=dw_sb[:], in_=dense_w.rearrange("(k p) n -> p k n", p=P))
         nc.sync.dma_start(out=db_row[0:1, :], in_=dense_b.rearrange("(o n) -> o n", o=1))
 
@@ -122,9 +126,8 @@ def tile_styleganlayerepilogue_kernel(
         w_scales = keep.tile([P, 512], U8, name="w_scales", align_bytes=64)
 
         def w_group(lo, hi):
-            nc.vector.tensor_copy(
-                out=w_grp[:, lo:hi, :], in_=w_raw[:, :, lo:hi].rearrange("p t c -> p c t")
-            )
+            src = w_raw0[:] if lo == 0 else w_raw1[:, :, lo - P : hi - P]
+            nc.vector.tensor_copy(out=w_grp[:, lo:hi, :], in_=src.rearrange("p t c -> p c t"))
 
         def w_quant(lo, hi):
             nc.vector.quantize_mx(
@@ -192,7 +195,7 @@ def tile_styleganlayerepilogue_kernel(
 
         def z_step(s):
             ct, g = s // NG, s % NG
-            z = work.tile([P, 512], F32, name="z", tag="z")
+            z = work.tile([P, 512], F32, name="z", tag="z", bufs=4)
             nc.vector.scalar_tensor_tensor(
                 out=z[:],
                 in0=nm_bc[g // 2][:, (g % 2) * 512 : (g % 2 + 1) * 512],
@@ -205,7 +208,7 @@ def tile_styleganlayerepilogue_kernel(
 
         def r_step(s):
             ct = s // NG
-            r = work.tile([P, 512], F32, name="r", tag="r")
+            r = work.tile([P, 512], F32, name="r", tag="r", bufs=4)
             nc.scalar.activation(
                 out=r[:], in_=z_t[s][:], func=ACT.Relu, bias=b4_col[:, ct : ct + 1], scale=4.0
             )
@@ -218,7 +221,7 @@ def tile_styleganlayerepilogue_kernel(
             y_t[s] = yt
 
         def q_step(s):
-            qt = work.tile([P, 512], F32, name="qt", tag="q")
+            qt = work.tile([P, 512], F32, name="qt", tag="q", bufs=6)
             nc.scalar.activation(out=qt[:], in_=y_t[s][:], func=ACT.Square)
             q_t[s] = qt
 
@@ -298,7 +301,7 @@ def tile_styleganlayerepilogue_kernel(
 
         def w_step(e):
             ct = e // NG
-            wt = work.tile([P, 4, P], F32, name="wt", tag="w", bufs=4)
+            wt = work.tile([P, 4, P], F32, name="wt", tag="w", bufs=5)
             nc.vector.tensor_tensor(
                 out=wt[:],
                 in0=y_t[e][:].rearrange("p (h b) -> p h b", h=4),
@@ -335,7 +338,7 @@ def tile_styleganlayerepilogue_kernel(
 
         def exit_step(e):
             ct, g = e // NG, e % NG
-            ot = work.tile([P, 4, P], F32, name="ot", tag="ot", bufs=6)
+            ot = work.tile([P, 4, P], F32, name="ot", tag="ot", bufs=12)
             if exit_on_vector(e):
                 nc.vector.tensor_tensor(
                     out=ot[:],
@@ -403,12 +406,19 @@ def tile_styleganlayerepilogue_kernel(
         x_turn(2, ("o", "o"))
         x_copy(2, 0, "s")
         noise_half(1)
-        for i in range(NSTEP + LAG + 2):
-            due = [(ct, i - (NG * ct + NG - 1)) for ct in range(NCT)]
-            conv = i < NSTEP
-            e_out = i - LAG - 2
-            if conv:
-                z_step(i)
+        for i in range(NSTEP + 14):
+            due = [(ct, i - STEP[NG * ct + NG - 1]) for ct in range(NCT)]
+            unit = UNITS[i] if i < NSTEP else None
+            y_due = [u for u in range(NSTEP) if i == STEP[u] + 1]
+            q_due = [u for u in range(NSTEP) if i == STEP[u] + 2 and u % NG != NG - 1]
+            q_close = [u for u in range(NSTEP) if i == STEP[u] + 1 and u % NG == NG - 1]
+            sy_due = [u for u in range(NSTEP) if i == max(STEP[u], u) + 2]
+            sq_due = [u for u in range(NSTEP) if i == max(STEP[u], u) + (3 if u % NG != NG - 1 else 2)]
+            w_due = [e for e in range(NSTEP) if i == e + 8]
+            t_due = [e for e in range(NSTEP) if i == e + 9]
+            e_due = [e for e in range(NSTEP) if i == e + 10]
+            if unit is not None:
+                z_step(unit)
             for ct, k in due:
                 if k == 3:
                     stats_var(ct)
@@ -417,7 +427,7 @@ def tile_styleganlayerepilogue_kernel(
             if i < 3:
                 x_quant(i + 1)
             if i + 1 < NSTEP:
-                mx(i + 1)
+                mx(UNITS[i + 1])
             if i == 0:
                 style_turn()
                 x_turn(3, ("sy", "sq"))
@@ -427,47 +437,47 @@ def tile_styleganlayerepilogue_kernel(
             if i in (1, 2):
                 for n in range(4 * i - 4, 4 * i):
                     style_mm(n)
-            if i < 3:
-                w_group((i + 1) * P, (i + 2) * P)
             if 1 <= i < 4:
-                w_quant(i * P, (i + 1) * P)
-            if 1 <= i <= NSTEP:
-                y_step(i - 1)
+                w_group((i - 0) * P, (i - -1) * P)
+            if 2 <= i < 5:
+                w_quant((i - 1) * P, (i - 0) * P)
+            for u in y_due:
+                y_step(u)
             for ct, k in due:
                 if k == 4:
                     stats_b(ct)
-            if 2 <= i < NSTEP + 2 and (i - 2) % NG != NG - 1:
-                q_step(i - 2)
-            if e_out >= 0 and not exit_on_vector(e_out):
-                exit_step(e_out)
+            for u in q_due:
+                q_step(u)
+            for e in e_due:
+                if not exit_on_vector(e):
+                    exit_step(e)
             for ct, k in due:
                 if k == 3:
                     stats_rstd(ct)
-            if conv:
-                r_step(i)
+            if unit is not None:
+                r_step(unit)
             if i == 0:
                 noise_copy(1)
                 style_copy()
                 x_copy(3, 0, "s")
-            if 1 <= i <= NSTEP and (i - 1) % NG == NG - 1:
-                q_step(i - 1)
-            if 2 <= i < NSTEP + 2:
-                sums(i - 2, 0)
-            if 3 <= i < NSTEP + 3 and (i - 3) % NG != NG - 1:
-                sums(i - 3, 1)
-            if 2 <= i < NSTEP + 2 and (i - 2) % NG == NG - 1:
-                sums(i - 2, 1)
+            for u in q_close:
+                q_step(u)
+            for u in sy_due:
+                sums(u, 0)
+            for u in sq_due:
+                sums(u, 1)
             for ct, k in due:
                 if k == 2:
                     stats_m(ct)
                 if k == 6:
                     stats_bt(ct)
-            if 0 <= i - LAG < NSTEP:
-                w_step(i - LAG)
-            if 0 <= i - LAG - 1 < NSTEP:
-                turn_out(i - LAG - 1, "o" if i < NSTEP or i % 2 == 0 else "p")
-            if e_out >= 0 and exit_on_vector(e_out):
-                exit_step(e_out)
+            for e in w_due:
+                w_step(e)
+            for e in t_due:
+                turn_out(e, "o" if i < NSTEP or i % 2 == 0 else "p")
+            for e in e_due:
+                if exit_on_vector(e):
+                    exit_step(e)
             for ct, k in due:
                 if k == 4:
                     stats_ta(ct)

@@ -92,7 +92,7 @@ def tile_styleganlayerepilogue_kernel(
 
         nw_col = keep.tile([P, NCT], F32, name="nw_col")
         b4_col = keep.tile([P, NCT], F32, name="b4_col")
-        nm_bc = [keep.tile([P, 1024], BF16, name="nm_bc%d" % h) for h in range(2)]
+        nm_bc = [keep.tile([P, 4, P], F32, name="nm_bc%d" % h) for h in range(2)]
 
         nm_t = {}
 
@@ -105,13 +105,12 @@ def tile_styleganlayerepilogue_kernel(
             )
 
         def noise_half(half):
-            nm_ps = ps.tile([P, 1024], BF16, name="nm_ps%d" % half, tag="ab", bufs=2)
-            for j in range(8):
-                hw = half * 8 + j
+            nm_ps = ps.tile([P, 4, P], F32, name="nm_ps%d" % half, tag="ab", bufs=2)
+            nmw = nm_sb[:].bitcast(F32)
+            for j in range(4):
+                w = half * 4 + j
                 nc.tensor.transpose(
-                    nm_ps[:, j * P : (j + 1) * P],
-                    nm_sb[:, hw : hw + 1].to_broadcast([P, P]),
-                    ident_b[:],
+                    nm_ps[:, j, :], nmw[:, w : w + 1].to_broadcast([P, P]), ident_f[:]
                 )
             nm_t[half] = nm_ps
 
@@ -167,7 +166,7 @@ def tile_styleganlayerepilogue_kernel(
 
         def x_copy(g, hh, eng):
             xgw = x_grp[g][:].bitcast(F32)
-            dst = xgw[:, hh * 512 : (hh + 1) * 512].rearrange("p (h b u) -> p h b u", h=2, u=2)
+            dst = xgw.rearrange("p (h q b u) -> p h q b u", h=2, q=2, u=2)[:, :, hh]
             src = xt_t[(g, hh)][:].rearrange("p (h u) b -> p h b u", h=2)
             if eng == "s":
                 nc.scalar.copy(out=dst, in_=src)
@@ -197,10 +196,13 @@ def tile_styleganlayerepilogue_kernel(
             ct, g = s // NG, s % NG
             z = work.tile([P, 512], F32, name="z", tag="z", bufs=4)
             nc.vector.scalar_tensor_tensor(
-                out=z[:],
-                in0=nm_bc[g // 2][:, (g % 2) * 512 : (g % 2 + 1) * 512],
+                out=z[:].rearrange("p (t n) -> p t n", t=2),
+                in0=nm_bc[g // 2][:, g % 2 * 2 : g % 2 * 2 + 2, :]
+                .rearrange("p j b -> p (j b)")
+                .bitcast(BF16)
+                .rearrange("p (n t) -> p t n", t=2),
                 scalar=nw_col[:, ct : ct + 1],
-                in1=acc_t[s][:],
+                in1=acc_t[s][:].rearrange("p (t n) -> p t n", t=2),
                 op0=ALU.mult,
                 op1=ALU.add,
             )
@@ -326,12 +328,12 @@ def tile_styleganlayerepilogue_kernel(
             add_b = not exit_on_vector(e) and not shift_on_gpsimd(e)
             for j in range(4):
                 nc.tensor.matmul(
-                    out=o_ps[:, j, :], lhsT=w_t[e][:, j, :], rhs=ident_f[:],
+                    out=o_ps[:, j % 2 * 2 + j // 2, :], lhsT=w_t[e][:, j, :], rhs=ident_f[:],
                     is_transpose=True, start=True, stop=not add_b,
                 )
                 if add_b:
                     nc.tensor.matmul(
-                        out=o_ps[:, j, :], lhsT=sm[("bT", ct)][:], rhs=ident_f[:],
+                        out=o_ps[:, j % 2 * 2 + j // 2, :], lhsT=sm[("bT", ct)][:], rhs=ident_f[:],
                         is_transpose=True, start=False, stop=True,
                     )
             o_t[e] = o_ps

@@ -25,7 +25,7 @@ STEP = [UNITS.index(u) for u in range(NSTEP)]
 
 
 def exit_on_vector(e):
-    return e % 2 == 0 or e > 12
+    return e % 2 == 0 or e == NSTEP - 1
 
 
 def shift_on_gpsimd(e):
@@ -61,10 +61,10 @@ def tile_styleganlayerepilogue_kernel(
         rows = keep.tile([P, P], BF16, name="rows")
         nc.vector.memset(rows[:].bitcast(I32), 0)
 
-        nc.sync.dma_start(out=nm_sb[:], in_=noise_map.rearrange("b h w o -> b (h w o)"))
         for half in range(2):
             cs = slice(half * 1024, (half + 1) * 1024)
             nc.sync.dma_start(out=x_sb[0][:, cs], in_=xv[:, cs])
+        nc.sync.dma_start(out=nm_sb[:], in_=noise_map.rearrange("b h w o -> b (h w o)"))
         wv = conv_w.rearrange("(p j) c -> p j c", j=4)
         nc.sync.dma_start(out=w_raw0[:], in_=wv[:, :, 0:P])
         nc.sync.dma_start(
@@ -408,28 +408,29 @@ def tile_styleganlayerepilogue_kernel(
         x_turn(2, ("o", "o"))
         x_copy(2, 0, "s")
         noise_half(1)
+        x_quant(1)
         for i in range(NSTEP + 14):
-            due = [(ct, i - STEP[NG * ct + NG - 1]) for ct in range(NCT)]
+            due = [(ct, i - STEP[NG * ct + NG - 1] - (0)) for ct in range(NCT)]
             unit = UNITS[i] if i < NSTEP else None
-            y_due = [u for u in range(NSTEP) if i == STEP[u] + 1]
-            q_due = [u for u in range(NSTEP) if i == STEP[u] + 2 and u % NG != NG - 1]
-            q_close = [u for u in range(NSTEP) if i == STEP[u] + 1 and u % NG == NG - 1]
-            sy_due = [u for u in range(NSTEP) if i == max(STEP[u], u) + 2]
-            sq_due = [u for u in range(NSTEP) if i == max(STEP[u], u) + (3 if u % NG != NG - 1 else 2)]
+            y_due = [u for u in range(NSTEP) if i == u + 1]
+            q_due = [u for u in range(NSTEP) if i == u + 2 and u % NG != NG - 1]
+            q_close = [u for u in range(NSTEP) if i == u + 1 and u % NG == NG - 1]
+            sy_due = [u for u in range(NSTEP) if i == u + 2]
+            sq_due = [u for u in range(NSTEP) if i == u + (3 if u % NG != NG - 1 else 2)]
             w_due = [e for e in range(NSTEP) if i == e + 8]
             t_due = [e for e in range(NSTEP) if i == e + 9]
             e_due = [e for e in range(NSTEP) if i == e + 10]
-            if unit is not None:
-                z_step(unit)
+            if i < 4:
+                z_step(i)
             for ct, k in due:
                 if k == 3:
                     stats_var(ct)
                 if k == 4:
                     stats_a(ct)
-            if i < 3:
+            if 0 < i < 3:
                 x_quant(i + 1)
-            if i + 1 < NSTEP:
-                mx(UNITS[i + 1])
+            if i + 1 < 4:
+                mx(i + 1)
             if i == 0:
                 style_turn()
                 x_turn(3, ("sy", "sq"))
@@ -437,7 +438,7 @@ def tile_styleganlayerepilogue_kernel(
             if i == 1:
                 x_copy(3, 1, "s")
             if i in (1, 2):
-                for n in range(4 * i - 4, 4 * i):
+                for n in range(5 * i - 5, min(5 * i, 8)):
                     style_mm(n)
             if 1 <= i < 4:
                 w_group((i - 0) * P, (i - -1) * P)
@@ -450,38 +451,49 @@ def tile_styleganlayerepilogue_kernel(
                     stats_b(ct)
             for u in q_due:
                 q_step(u)
-            for e in e_due:
-                if not exit_on_vector(e):
-                    exit_step(e)
             for ct, k in due:
                 if k == 3:
                     stats_rstd(ct)
             if unit is not None:
                 r_step(unit)
+            for e in e_due:
+                if not exit_on_vector(e):
+                    exit_step(e)
             if i == 0:
                 noise_copy(1)
                 style_copy()
                 x_copy(3, 0, "s")
             for u in q_close:
                 q_step(u)
+            for u in sq_due:
+                if u % NG != NG - 1:
+                    sums(u, 1)
             for u in sy_due:
                 sums(u, 0)
-            for u in sq_due:
-                sums(u, 1)
             for ct, k in due:
                 if k == 2:
                     stats_m(ct)
+            for u in sq_due:
+                if u % NG == NG - 1:
+                    sums(u, 1)
+            for ct, k in due:
                 if k == 6:
                     stats_bt(ct)
             for e in w_due:
                 w_step(e)
+            if 4 <= i + 1 < NSTEP:
+                z_step(i + 1)
+            if i == NSTEP + 3:
+                stats_ta(NCT - 1)
             for e in t_due:
                 turn_out(e, "o" if i < NSTEP or i % 2 == 0 else "p")
+            if 4 <= i + 2 < NSTEP:
+                mx(i + 2)
             for e in e_due:
                 if exit_on_vector(e):
                     exit_step(e)
             for ct, k in due:
-                if k == 4:
+                if k == 4 and ct < NCT - 1:
                     stats_ta(ct)
                 if k == 5:
                     stats_tb(ct)

from contextlib import ExitStack

import concourse.mybir as mybir
from concourse.masks import make_identity

FLOPS = 2 * 2048 * 512 * 512 + 2 * 128 * 512 * 1024

F32 = mybir.dt.float32
BF16 = mybir.dt.bfloat16
U32 = mybir.dt.uint32
U8 = mybir.dt.uint8
I32 = mybir.dt.int32
FP8X4 = mybir.dt.float8_e4m3fn_x4
ALU = mybir.AluOpType
ACT = mybir.ActivationFunctionType

P = 128
HW = 16
NG = 4
NCT = 4
NSTEP = NG * NCT
EPS = 1e-8
UNITS = list(range(NSTEP))
STEP = [UNITS.index(u) for u in range(NSTEP)]


def exit_on_vector(e):
    return e % 2 == 0 or e == NSTEP - 1


def shift_on_gpsimd(e):
    return False


def y_on_vector(s):
    return s < 8 or s % NG == NG - 1


def tile_styleganlayerepilogue_kernel(
    tc, x, dlatents, noise_map, conv_w, noise_weight, bias, dense_w, dense_b, out
):
    nc = tc.nc
    with ExitStack() as ctx:
        keep = ctx.enter_context(tc.tile_pool(name="keep", bufs=1))
        work = ctx.enter_context(tc.tile_pool(name="work", bufs=3))
        small = ctx.enter_context(tc.tile_pool(name="small", bufs=2))
        ps = ctx.enter_context(tc.psum_pool(name="ps", bufs=1))

        xv = x.rearrange("b h w c -> b (h w c)")
        x_sb = [keep.tile([P, 2048], BF16, name="x_sb%d" % g) for g in range(NG)]
        w_raw0 = keep.tile([P, 4, P], BF16, name="w_raw0")
        w_raw1 = keep.tile([P, 4, 384], BF16, name="w_raw1")
        nm_sb = keep.tile([P, HW], BF16, name="nm_sb")
        dl_sb = keep.tile([P, 512], BF16, name="dl_sb")
        dw_sb = keep.tile([P, 4, 1024], BF16, name="dw_sb")
        db_row = keep.tile([P, 1024], BF16, name="db_row")
        nc.gpsimd.memset(db_row[:], 0.0)
        ones_row = keep.tile([P, P], BF16, name="ones_row")
        nc.gpsimd.memset(ones_row[:], 0.0)
        nc.gpsimd.memset(ones_row[0:1, :], 1.0)
        rows = keep.tile([P, P], BF16, name="rows")
        nc.vector.memset(rows[:].bitcast(I32), 0)

        for half in range(2):
            cs = slice(half * 1024, (half + 1) * 1024)
            nc.sync.dma_start(out=x_sb[0][:, cs], in_=xv[:, cs])
        nc.sync.dma_start(out=nm_sb[:], in_=noise_map.rearrange("b h w o -> b (h w o)"))
        wv = conv_w.rearrange("(p j) c -> p j c", j=4)
        nc.sync.dma_start(out=w_raw0[:], in_=wv[:, :, 0:P])
        nc.sync.dma_start(
            out=rows[0:4, :], in_=noise_weight.rearrange("a b c (r n) -> (a b c r) n", r=4)
        )
        nc.sync.dma_start(out=rows[4:8, :], in_=bias.rearrange("a b c (r n) -> (a b c r) n", r=4))
        nc.sync.dma_start(out=x_sb[1][:], in_=xv[:, 2048:4096])
        nc.sync.dma_start(out=dl_sb[:], in_=dlatents)
        nc.sync.dma_start(out=x_sb[2][:], in_=xv[:, 4096:6144])
        nc.sync.dma_start(out=w_raw1[:], in_=wv[:, :, P:512])
        nc.sync.dma_start(out=x_sb[3][:], in_=xv[:, 6144:8192])
        nc.sync.dma_start(out=dw_sb[:], in_=dense_w.rearrange("(k p) n -> p k n", p=P))
        nc.sync.dma_start(out=db_row[0:1, :], in_=dense_b.rearrange("(o n) -> o n", o=1))

        warm = keep.tile([P, 1], F32, name="warm")
        nc.vector.memset(warm[:], 1.0)
        ident_b = keep.tile([P, P], BF16, name="ident_b")
        make_identity(nc, ident_b[:])
        ident_f = keep.tile([P, P], F32, name="ident_f")
        make_identity(nc, ident_f[:])
        warm2 = keep.tile([P, 1], F32, name="warm2")
        eps_t = keep.tile([P, 1], F32, name="eps_t")
        nc.vector.memset(eps_t[:], 25.0 * EPS)
        nc.scalar.activation(out=warm2[:], in_=warm[:], func=ACT.Abs_reciprocal_sqrt)

        nw_col = keep.tile([P, NCT], F32, name="nw_col")
        b4_col = keep.tile([P, NCT], F32, name="b4_col")
        nm_bc = [keep.tile([P, 4, P], F32, name="nm_bc%d" % h) for h in range(2)]

        nm_t = {}

        def columns():
            cols_ps = ps.tile([P, P], BF16, name="cols_ps", tag="p", bufs=2)
            nc.tensor.transpose(cols_ps[:], rows[:], ident_b[:])
            nc.vector.tensor_copy(out=nw_col[:], in_=cols_ps[:, 0:4])
            nc.vector.tensor_scalar(
                out=b4_col[:], in0=cols_ps[:, 4:8], scalar1=4.0, scalar2=None, op0=ALU.mult
            )

        def noise_half(half):
            nm_ps = ps.tile([P, 4, P], F32, name="nm_ps%d" % half, tag="ab", bufs=2)
            nmw = nm_sb[:].bitcast(F32)
            for j in range(4):
                w = half * 4 + j
                nc.tensor.transpose(
                    nm_ps[:, j, :], nmw[:, w : w + 1].to_broadcast([P, P]), ident_f[:]
                )
            nm_t[half] = nm_ps

        def noise_copy(half):
            if half == 0:
                nc.vector.tensor_copy(out=nm_bc[half][:], in_=nm_t[half][:])
            else:
                nc.scalar.copy(out=nm_bc[half][:], in_=nm_t[half][:])

        w_grp = keep.tile([P, 512, 4], BF16, name="w_grp", align_bytes=64)
        w_codes = keep.tile([P, 512], U32, name="w_codes", align_bytes=64)
        w_scales = keep.tile([P, 512], U8, name="w_scales", align_bytes=64)

        def w_group(lo, hi):
            src = w_raw0[:] if lo == 0 else w_raw1[:, :, lo - P : hi - P]
            nc.vector.tensor_copy(out=w_grp[:, lo:hi, :], in_=src.rearrange("p t c -> p c t"))

        def w_quant(lo, hi):
            nc.vector.quantize_mx(
                out=w_codes[:, lo:hi].bitcast(FP8X4),
                scales=w_scales[:, lo:hi],
                in_=w_grp[:, lo:hi, :].rearrange("p c t -> p (c t)"),
            )

        x_grp = [keep.tile([P, 2048], BF16, name="x_grp%d" % g, align_bytes=64) for g in range(NG)]
        x_codes = [keep.tile([P, 512], U32, name="x_codes%d" % g, align_bytes=64) for g in range(NG)]
        x_scales = [keep.tile([P, 512], U8, name="x_scales%d" % g, align_bytes=64) for g in range(NG)]
        outv = out.rearrange("b h w c -> b (h w) c")
        xt_t = {}
        acc_t = {}
        z_t = {}
        r_t = {}
        y_t = {}
        q_t = {}
        w_t = {}
        o_t = {}
        sum_t = {}
        sm = {}
        gb_sb = [keep.tile([P, 512], F32, name="gb_sb%d" % h) for h in range(2)]
        dlT = keep.tile([P, 4, P], BF16, name="dlT")

        def x_turn(g, tags):
            xw = x_sb[g][:].bitcast(F32)
            for hh in range(2):
                tag = tags[hh]
                xt = ps.tile([P, 4, P], F32, name="xt", tag=tag, bufs=(1 if tag[0] == "s" else 2))
                for j in range(4):
                    px, u = hh * 2 + j // 2, j % 2
                    nc.tensor.transpose(
                        xt[:, j, :], xw[:, px * 256 + u : (px + 1) * 256 : 2], ident_f[:]
                    )
                xt_t[(g, hh)] = xt

        def x_copy(g, hh, eng):
            xgw = x_grp[g][:].bitcast(F32)
            dst = xgw.rearrange("p (h q b u) -> p h q b u", h=2, q=2, u=2)[:, :, hh]
            src = xt_t[(g, hh)][:].rearrange("p (h u) b -> p h b u", h=2)
            if eng == "s":
                nc.scalar.copy(out=dst, in_=src)
            else:
                nc.vector.tensor_copy(out=dst, in_=src)

        def x_quant(g):
            nc.vector.quantize_mx(
                out=x_codes[g][:].bitcast(FP8X4), scales=x_scales[g][:], in_=x_grp[g][:]
            )

        def mx(s):
            ct, g = s // NG, s % NG
            acc = ps.tile([P, 512], F32, name="acc", tag="p", bufs=2)
            nc.tensor.matmul_mx(
                out=acc[:],
                lhsT=w_codes[:, ct * P : (ct + 1) * P].bitcast(FP8X4),
                lhsT_scale=w_scales[:, ct * P : (ct + 1) * P],
                rhs=x_codes[g][:].bitcast(FP8X4),
                rhs_scale=x_scales[g][:],
                start=True,
                stop=True,
            )
            acc_t[s] = acc

        def z_step(s):
            ct, g = s // NG, s % NG
            z = work.tile([P, 512], F32, name="z", tag="z", bufs=4)
            nc.vector.scalar_tensor_tensor(
                out=z[:].rearrange("p (t n) -> p t n", t=2),
                in0=nm_bc[g // 2][:, g % 2 * 2 : g % 2 * 2 + 2, :]
                .rearrange("p j b -> p (j b)")
                .bitcast(BF16)
                .rearrange("p (n t) -> p t n", t=2),
                scalar=nw_col[:, ct : ct + 1],
                in1=acc_t[s][:].rearrange("p (t n) -> p t n", t=2),
                op0=ALU.mult,
                op1=ALU.add,
            )
            z_t[s] = z

        def r_step(s):
            ct = s // NG
            r = work.tile([P, 512], F32, name="r", tag="r", bufs=4)
            nc.scalar.activation(
                out=r[:], in_=z_t[s][:], func=ACT.Relu, bias=b4_col[:, ct : ct + 1], scale=4.0
            )
            r_t[s] = r

        def y_step(s):
            yt = keep.tile([P, 512], F32, name="y%d" % s)
            eng = nc.vector if y_on_vector(s) else nc.gpsimd
            eng.tensor_tensor(out=yt[:], in0=z_t[s][:], in1=r_t[s][:], op=ALU.add)
            y_t[s] = yt

        def q_step(s):
            qt = work.tile([P, 512], F32, name="qt", tag="q", bufs=6)
            nc.scalar.activation(out=qt[:], in_=y_t[s][:], func=ACT.Square)
            q_t[s] = qt

        def sums(s, k):
            ct, g = s // NG, s % NG
            if g == 0:
                sum_t[(ct, k)] = ps.tile([P, P], F32, name="acc_sum", tag=("sy" if k == 0 else "sq"))
            src = y_t[s] if k == 0 else q_t[s]
            for j in range(4):
                hw = g * 4 + j
                nc.tensor.matmul(
                    out=sum_t[(ct, k)][:],
                    lhsT=src[:, j * P : (j + 1) * P],
                    rhs=ident_f[:],
                    is_transpose=True,
                    start=(hw == 0),
                    stop=(hw == HW - 1),
                )

        def stats_m(ct):
            msq = small.tile([P, P], F32, name="msq", tag="msq")
            nc.scalar.activation(out=msq[:], in_=sum_t[(ct, 0)][:], func=ACT.Square)
            mean = small.tile([P, P], F32, name="mean", tag="mean")
            nc.scalar.activation(
                out=mean[:], in_=sum_t[(ct, 0)][:], func=ACT.Copy, scale=1.0 / HW
            )
            sm[("mean", ct)] = mean
            sm[("msq", ct)] = msq

        def stats_var(ct):
            var = small.tile([P, P], F32, name="var", tag="var")
            nc.vector.scalar_tensor_tensor(
                out=var[:], in0=sum_t[(ct, 1)][:], scalar=float(HW), in1=sm[("msq", ct)][:],
                op0=ALU.mult, op1=ALU.subtract,
            )
            sm[("var", ct)] = var

        def stats_rstd(ct):
            rstd = small.tile([P, P], F32, name="rstd", tag="rstd")
            nc.scalar.activation(
                out=rstd[:], in_=sm[("var", ct)][:], func=ACT.Abs_reciprocal_sqrt, bias=eps_t[:],
                scale=1.0 / (HW * HW),
            )
            sm[("rstd", ct)] = rstd

        def stats_a(ct):
            cs = slice(ct * P, (ct + 1) * P)
            a = small.tile([P, P], F32, name="a", tag="a")
            nc.gpsimd.tensor_tensor(out=a[:], in0=sm[("rstd", ct)][:], in1=gb_sb[0][:, cs], op=ALU.mult)
            sm[("a", ct)] = a

        def stats_b(ct):
            cs = slice(ct * P, (ct + 1) * P)
            eng = nc.gpsimd
            ma = small.tile([P, P], F32, name="ma", tag="ma")
            eng.tensor_tensor(out=ma[:], in0=sm[("mean", ct)][:], in1=sm[("a", ct)][:], op=ALU.mult)
            b = small.tile([P, P], F32, name="b", tag="b")
            eng.tensor_tensor(out=b[:], in0=gb_sb[1][:, cs], in1=ma[:], op=ALU.subtract)
            sm[("b", ct)] = b

        def stats_ta(ct):
            tag, bufs = ("sy", 1) if ct == NCT - 1 else ("ab", 2)
            a_ps = ps.tile([P, P], F32, name="a_ps", tag=tag, bufs=bufs)
            nc.tensor.transpose(a_ps[:], sm[("a", ct)][:], ident_f[:])
            sm[("aT", ct)] = a_ps

        def stats_tb(ct):
            tag, bufs = ("sq", 1) if ct == NCT - 1 else ("ab", 2)
            b_ps = ps.tile([P, P], F32, name="b_ps", tag=tag, bufs=bufs)
            nc.tensor.transpose(b_ps[:], sm[("b", ct)][:], ident_f[:])
            sm[("b_ps", ct)] = b_ps

        def stats_bt(ct):
            bT = small.tile([P, P], F32, name="bT", tag="bT")
            nc.scalar.copy(out=bT[:], in_=sm[("b_ps", ct)][:])
            sm[("bT", ct)] = bT

        def w_step(e):
            ct = e // NG
            wt = work.tile([P, 4, P], F32, name="wt", tag="w", bufs=5)
            nc.vector.tensor_tensor(
                out=wt[:],
                in0=y_t[e][:].rearrange("p (h b) -> p h b", h=4),
                in1=sm[("aT", ct)][:].unsqueeze(1).to_broadcast([P, 4, P]),
                op=ALU.mult,
            )
            w_t[e] = wt

        def turn_out(e, tag="o"):
            ct = e // NG
            o_ps = ps.tile([P, 4, P], F32, name="o_ps", tag=tag, bufs=2)
            if e >= 8 and e % 2 == 0:
                nc.tensor.matmul_mx(
                    out=o_ps[:].rearrange("p h c -> p (h c)"),
                    lhsT=w_codes[:, 0:P].bitcast(FP8X4),
                    lhsT_scale=w_scales[:, 0:P],
                    rhs=x_codes[0][:].bitcast(FP8X4),
                    rhs_scale=x_scales[0][:],
                    start=True,
                    stop=True,
                )
            add_b = not exit_on_vector(e) and not shift_on_gpsimd(e)
            for j in range(4):
                nc.tensor.matmul(
                    out=o_ps[:, j % 2 * 2 + j // 2, :], lhsT=w_t[e][:, j, :], rhs=ident_f[:],
                    is_transpose=True, start=True, stop=not add_b,
                )
                if add_b:
                    nc.tensor.matmul(
                        out=o_ps[:, j % 2 * 2 + j // 2, :], lhsT=sm[("bT", ct)][:], rhs=ident_f[:],
                        is_transpose=True, start=False, stop=True,
                    )
            o_t[e] = o_ps

        def exit_step(e):
            ct, g = e // NG, e % NG
            ot = work.tile([P, 4, P], F32, name="ot", tag="ot", bufs=12)
            if exit_on_vector(e):
                nc.vector.tensor_tensor(
                    out=ot[:],
                    in0=o_t[e][:],
                    in1=sm[("b", ct)][:].unsqueeze(1).to_broadcast([P, 4, P]),
                    op=ALU.add,
                )
            elif shift_on_gpsimd(e):
                ev = work.tile([P, 4, P], F32, name="ev", tag="ev")
                nc.scalar.copy(out=ev[:], in_=o_t[e][:])
                nc.gpsimd.tensor_tensor(
                    out=ot[:],
                    in0=ev[:],
                    in1=sm[("b", ct)][:].unsqueeze(1).to_broadcast([P, 4, P]),
                    op=ALU.add,
                )
            else:
                nc.scalar.copy(out=ot[:], in_=o_t[e][:])
            nc.sync.dma_start(out=outv[:, g * 4 : (g + 1) * 4, ct * P : (ct + 1) * P], in_=ot[:])

        def style_turn():
            dlT_ps = ps.tile([P, 4, P], BF16, name="dlT_ps", tag="p", bufs=2)
            for kc in range(4):
                nc.tensor.transpose(dlT_ps[:, kc, :], dl_sb[:, kc * P : (kc + 1) * P], ident_b[:])
            sm["dlT_ps"] = dlT_ps

        def style_copy():
            nc.scalar.copy(out=dlT[:], in_=sm["dlT_ps"][:])

        def style_mm(n):
            half, kc = n // 4, n % 4
            cs = slice(half * 512, (half + 1) * 512)
            if kc == 0:
                sm[("gb", half)] = ps.tile([P, 512], F32, name="gb_ps", tag="ab", bufs=2)
            nc.tensor.matmul(
                out=sm[("gb", half)][:], lhsT=dlT[:, kc, :], rhs=dw_sb[:, kc, cs],
                start=(kc == 0), stop=False,
            )
            if kc == 3:
                nc.tensor.matmul(
                    out=sm[("gb", half)][:], lhsT=ones_row[:], rhs=db_row[:, cs],
                    start=False, stop=True,
                )

        def style_out(half):
            nc.scalar.activation(
                out=gb_sb[half][:], in_=sm[("gb", half)][:], func=ACT.Identity,
                bias=(1.0 if half == 0 else 0.0), scale=1.0,
            )

        ctx.enter_context(tc.manual_schedule())
        x_turn(0, ("o", "o"))
        x_copy(0, 0, "v")
        x_copy(0, 1, "s")
        w_group(0, P)
        w_quant(0, P)
        x_quant(0)
        noise_half(0)
        noise_copy(0)
        columns()
        x_turn(1, ("sy", "sq"))
        mx(0)
        x_copy(1, 0, "s")
        x_copy(1, 1, "s")
        x_turn(2, ("o", "o"))
        x_copy(2, 0, "s")
        noise_half(1)
        x_quant(1)
        for i in range(NSTEP + 14):
            due = [(ct, i - STEP[NG * ct + NG - 1] - (0)) for ct in range(NCT)]
            unit = UNITS[i] if i < NSTEP else None
            y_due = [u for u in range(NSTEP) if i == u + 1]
            q_due = [u for u in range(NSTEP) if i == u + 2 and u % NG != NG - 1]
            q_close = [u for u in range(NSTEP) if i == u + 1 and u % NG == NG - 1]
            sy_due = [u for u in range(NSTEP) if i == u + 2]
            sq_due = [u for u in range(NSTEP) if i == u + (3 if u % NG != NG - 1 else 2)]
            w_due = [e for e in range(NSTEP) if i == e + 8]
            t_due = [e for e in range(NSTEP) if i == e + 9]
            e_due = [e for e in range(NSTEP) if i == e + 10]
            if i < 4:
                z_step(i)
            for ct, k in due:
                if k == 3:
                    stats_var(ct)
                if k == 4:
                    stats_a(ct)
            if 0 < i < 3:
                x_quant(i + 1)
            if i + 1 < 4:
                mx(i + 1)
            if i == 0:
                style_turn()
                x_turn(3, ("sy", "sq"))
                x_copy(2, 1, "v")
            if i == 1:
                x_copy(3, 1, "s")
            if i in (1, 2):
                for n in range(5 * i - 5, min(5 * i, 8)):
                    style_mm(n)
            if 1 <= i < 4:
                w_group((i - 0) * P, (i - -1) * P)
            if 2 <= i < 5:
                w_quant((i - 1) * P, (i - 0) * P)
            for u in y_due:
                y_step(u)
            for ct, k in due:
                if k == 4:
                    stats_b(ct)
            for u in q_due:
                q_step(u)
            for ct, k in due:
                if k == 3:
                    stats_rstd(ct)
            if unit is not None:
                r_step(unit)
            for e in e_due:
                if not exit_on_vector(e):
                    exit_step(e)
            if i == 0:
                noise_copy(1)
                style_copy()
                x_copy(3, 0, "s")
            for u in q_close:
                q_step(u)
            for u in sq_due:
                if u % NG != NG - 1:
                    sums(u, 1)
            for u in sy_due:
                sums(u, 0)
            for ct, k in due:
                if k == 2:
                    stats_m(ct)
            for u in sq_due:
                if u % NG == NG - 1:
                    sums(u, 1)
            for ct, k in due:
                if k == 6:
                    stats_bt(ct)
            for e in w_due:
                w_step(e)
            if 4 <= i + 1 < NSTEP:
                z_step(i + 1)
            if i == NSTEP + 3:
                stats_ta(NCT - 1)
            for e in t_due:
                turn_out(e, "o" if i < NSTEP or i % 2 == 0 else "p")
            if 4 <= i + 2 < NSTEP:
                mx(i + 2)
            for e in e_due:
                if exit_on_vector(e):
                    exit_step(e)
            for ct, k in due:
                if k == 4 and ct < NCT - 1:
                    stats_ta(ct)
                if k == 5:
                    stats_tb(ct)
            if i in (2, 3):
                style_out(i - 2)
